import numpy as np
import ml_dtypes


def mxq(x, axis, fmt="e4m3"):
    dtype, down = {"e4m3": (ml_dtypes.float8_e4m3fn, 7), "e5m2": (ml_dtypes.float8_e5m2, 14)}[fmt]
    v = np.moveaxis(np.asarray(x, np.float32).astype(ml_dtypes.bfloat16).astype(np.float64), axis, -1)
    blocks = v.reshape(v.shape[:-1] + (-1, 32))
    amax = np.abs(blocks).max(-1, keepdims=True)
    byte = np.maximum(np.where(amax > 0, np.frexp(amax)[1] - 1 + 127, 0) - down, 1)
    scale = np.exp2(byte - 127.0)
    codes = (blocks / scale).astype(np.float32).astype(dtype).astype(np.float64)
    return np.moveaxis((codes * scale).reshape(v.shape), -1, axis)


WIDE = False


def mx_kscale(k):
    if not WIDE:
        return np.ones(k)
    levels = np.array([10, -10, 5, -5, 0])
    a = np.random.permutation(np.resize(levels, k // 512 * 4)).reshape(k // 512, 4)
    idx = np.arange(k)
    return np.exp2(a[idx // 512, idx % 128 // 32])


BF16 = ml_dtypes.bfloat16


def bf(x):
    return np.asarray(x, np.float32).astype(BF16)


def f64(x):
    return np.asarray(x).astype(np.float64)


B, D_IN, H1, H2, H3, C = 1024, 2048, 2048, 2048, 1024, 1024
BN_EPS = 1e-5


def bn_relu(z, gamma, beta):
    m = z.mean(axis=0)
    v = z.var(axis=0)
    return np.maximum((z - m) * (1.0 / np.sqrt(v + BN_EPS)) * gamma + beta, 0.0)


def setup_inputs():
    t = mx_kscale(H3)
    c = 32.0 * np.exp2(-15.0 * np.random.random(H3))
    mu = 0.5 * np.random.standard_normal(H3)
    return {"z2": bf((np.random.standard_normal((B, H3)) + mu) * c),
            "g2": bf((1.0 + 0.1 * np.random.standard_normal(H3)) * t),
            "beta2": bf(0.2 * np.random.standard_normal(H3) * t),
            "W3": bf(np.random.standard_normal((C, H3)) * 3.0 / np.sqrt(H3) / t),
            "b3": bf(0.5 * np.random.standard_normal(C))}


def reference(z2, g2, beta2, W3, b3):
    h = bn_relu(f64(z2), f64(g2), f64(beta2))
    logits = (mxq(h, 1, "e4m3") @ mxq(f64(W3), 1, "e4m3").T) + f64(b3)
    s = logits - logits.max(axis=1, keepdims=True)
    return s - np.log(np.exp(s).sum(axis=1, keepdims=True))

@@ -1,0 +1,272 @@
+from contextlib import ExitStack
+
+import concourse.mybir as mybir
+from concourse.masks import make_identity
+
+FLOPS = 2 * 1024 * 1024 * 1024
+
+F32 = mybir.dt.float32
+BF16 = mybir.dt.bfloat16
+U32 = mybir.dt.uint32
+U8 = mybir.dt.uint8
+FP8X4 = mybir.dt.float8_e4m3fn_x4
+ALU = mybir.AluOpType
+ACT = mybir.ActivationFunctionType
+AX = mybir.AxisListType
+
+P = 128
+B = 1024
+K = 1024
+C = 1024
+NT = B // P
+BN_EPS = 1e-5
+BF16_MAX = 3.3895313892515355e38
+
+
+def tile_binarymlp_pb_kernel(tc, z2, g2, beta2, W3, b3, out):
+    nc = tc.nc
+    with ExitStack() as ctx:
+        ctx.enter_context(tc.manual_schedule())
+        keep = ctx.enter_context(tc.tile_pool(name="keep", bufs=1))
+        rows = ctx.enter_context(tc.tile_pool(name="rows", bufs=NT))
+        junk = ctx.enter_context(tc.tile_pool(name="junk", bufs=2))
+        psum = ctx.enter_context(tc.psum_pool(name="psum", bufs=8))
+
+        ident = keep.tile([P, P], F32, name="ident")
+        make_identity(nc, ident[:])
+        one = keep.tile([P, 1], F32, name="one")
+        nc.vector.memset(one[:], 1.0)
+        warm = keep.tile([P, 1], F32, name="warm")
+        nc.scalar.activation(out=warm[:], in_=one[:], func=ACT.Sqrt)
+
+        z_nat = keep.tile([P, NT, K], BF16, name="z_nat")
+        z_view = z2.rearrange("(p t) f -> p t f", t=NT)
+        for c in range(4):
+            nc.sync.dma_start(out=z_nat[:, 2 * c : 2 * c + 2, :], in_=z_view[:, 2 * c : 2 * c + 2, :])
+        gamma = keep.tile([P, 8], BF16, name="gamma")
+        beta = keep.tile([P, 8], BF16, name="beta")
+        with nc.allow_non_contiguous_dma(reason="two small vectors, a pair of features to a partition"):
+            nc.sync.dma_start(
+                out=gamma[:].rearrange("p (v e) -> p v e", e=2),
+                in_=g2.rearrange("(v q e) -> q v e", v=4, e=2),
+            )
+            nc.sync.dma_start(
+                out=beta[:].rearrange("p (v e) -> p v e", e=2),
+                in_=beta2.rearrange("(v q e) -> q v e", v=4, e=2),
+            )
+        w_nat = keep.tile([P, NT, K], BF16, name="w_nat")
+        w_view = W3.rearrange("(j p) f -> p j f", p=P)
+        for c in range(4):
+            nc.sync.dma_start(out=w_nat[:, 2 * c : 2 * c + 2, :], in_=w_view[:, 2 * c : 2 * c + 2, :])
+        bias = keep.tile([P, C], BF16, name="bias")
+        nc.sync.dma_start(out=bias[:], in_=b3.partition_broadcast(P))
+
+        zw = keep.tile([P, 4 * B], F32, name="zw")
+        zw3 = zw[:].rearrange("p (v b) -> p v b", v=4)
+        zwb = zw[:].bitcast(BF16)
+        zw4 = zwb.rearrange("p (v b e) -> p v b e", v=4, e=2)
+        st = keep.tile([P, 4, 4, 6], F32, name="st")
+        mv = keep.tile([P, 8, 2], F32, name="mv")
+        vare = keep.tile([P, 8], F32, name="vare")
+        std = keep.tile([P, 8], F32, name="std")
+        rstd = keep.tile([P, 8], F32, name="rstd")
+        sc = keep.tile([P, 8], F32, name="sc")
+        msc = keep.tile([P, 8], F32, name="msc")
+        bi = keep.tile([P, 8], F32, name="bi")
+        wg = keep.tile([P, 2 * C * 4], BF16, name="wg", align_bytes=64)
+        wg_words = wg[:].bitcast(F32).rearrange("p (g c u) -> p g c u", g=2, u=2)
+        wq = keep.tile([P, 2 * C], U32, name="wq", align_bytes=64)
+        ws = keep.tile([P, 2 * C], U8, name="ws", align_bytes=64)
+        hT = keep.tile([P, 8, B], BF16, name="hT")
+        hg = keep.tile([P, 2 * B * 4], BF16, name="hg", align_bytes=64)
+        hq = keep.tile([P, 2 * B], U32, name="hq", align_bytes=64)
+        hs = keep.tile([P, 2 * B], U8, name="hs", align_bytes=64)
+        negm = keep.tile([P, NT], F32, name="negm")
+        sums = keep.tile([P, NT], F32, name="sums")
+        lns = keep.tile([P, NT], F32, name="lns")
+        negc_a = keep.tile([P, NT], F32, name="negc_a")
+        negc_b = keep.tile([P, NT], F32, name="negc_b")
+        out_view = out.rearrange("(p t) c -> t p c", t=NT)
+
+        def z_bank(jj, g):
+            zbank = psum.tile([P, 512], F32, tag="bank", name="zbank")
+            for u in range(2):
+                for jl in range(2):
+                    v = 2 * g + u
+                    nc.tensor.transpose(
+                        zbank[:, 256 * u + 128 * jl : 256 * u + 128 * jl + 128],
+                        z_nat[:, 2 * jj + jl, :].bitcast(F32)[:, 128 * v : 128 * v + 128],
+                        ident[:],
+                    )
+            nc.scalar.copy(
+                out=zw3[:, 2 * g : 2 * g + 2, 256 * jj : 256 * jj + 256],
+                in_=zbank[:].rearrange("p (u b) -> p u b", u=2),
+            )
+
+        def stats(jj, g):
+            for u in range(2):
+                v = 2 * g + u
+                lo = 2 * (v * B + 256 * jj)
+                nc.vector.bn_stats(out=st[:, v, jj, :], in_=zwb[:, lo : lo + 512])
+
+        def aggregate(g):
+            for u in range(2):
+                for e in range(2):
+                    v = 2 * g + u
+                    nc.vector.bn_aggr(out=mv[:, 2 * v + e, :], in_=st[:, v, :, 3 * e : 3 * e + 3])
+            cs = slice(4 * g, 4 * g + 4)
+            nc.vector.tensor_scalar(out=vare[:, cs], in0=mv[:, cs, 1], scalar1=BN_EPS, scalar2=None, op0=ALU.add)
+
+        def root(g):
+            cs = slice(4 * g, 4 * g + 4)
+            nc.scalar.activation(out=std[:, cs], in_=vare[:, cs], func=ACT.Sqrt)
+
+        def chain(g):
+            cs = slice(4 * g, 4 * g + 4)
+            nc.vector.reciprocal(out=rstd[:, cs], in_=std[:, cs])
+            nc.vector.tensor_tensor(out=sc[:, cs], in0=gamma[:, cs], in1=rstd[:, cs], op=ALU.mult)
+            nc.vector.tensor_tensor(out=msc[:, cs], in0=mv[:, cs, 0], in1=sc[:, cs], op=ALU.mult)
+            nc.vector.tensor_tensor(out=bi[:, cs], in0=beta[:, cs], in1=msc[:, cs], op=ALU.subtract)
+
+        def w_bank(j):
+            wbank = psum.tile([P, 512], F32, tag="bank", name="wbank")
+            for v in range(4):
+                nc.tensor.transpose(
+                    wbank[:, 128 * v : 128 * v + 128],
+                    w_nat[:, j, :].bitcast(F32)[:, 128 * v : 128 * v + 128],
+                    ident[:],
+                )
+            nc.scalar.copy(
+                out=wg_words[:, :, 128 * j : 128 * j + 128, :],
+                in_=wbank[:].rearrange("p (g u c) -> p g c u", g=2, u=2),
+            )
+
+        def w_quant(n):
+            for g in range(2):
+                lo = g * C + 512 * n
+                nc.vector.quantize_mx(
+                    out=wq[:, lo : lo + 512].bitcast(FP8X4),
+                    scales=ws[:, lo : lo + 512],
+                    in_=wg[:, 4 * lo : 4 * lo + 2048],
+                )
+
+        def norm(engine, g, r, ts):
+            bs = slice(512 * r, 512 * r + 512)
+            for t in ts:
+                c = 4 * g + t
+                src = zw4[:, c // 2, bs, c % 2]
+                if engine == "s":
+                    nc.scalar.activation(
+                        out=hT[:, c, bs], in_=src, func=ACT.Relu, bias=bi[:, c : c + 1], scale=sc[:, c : c + 1]
+                    )
+                else:
+                    nc.gpsimd.tensor_scalar(
+                        out=hT[:, c, bs], in0=src, scalar1=sc[:, c : c + 1], scalar2=bi[:, c : c + 1],
+                        op0=ALU.mult, op1=ALU.add,
+                    )
+
+        def regroup(engine, g, r):
+            lo = g * B + 512 * r
+            dst = hg[:, 4 * lo : 4 * lo + 2048].rearrange("p (c i t) -> p c t i", i=4, t=4)
+            src = hT[:, 4 * g : 4 * g + 4, 512 * r : 512 * r + 512].rearrange("p t (c i) -> p c t i", i=4)
+            if engine == "v":
+                nc.vector.tensor_scalar(out=dst, in0=src, scalar1=0.0, scalar2=None, op0=ALU.max)
+            else:
+                nc.gpsimd.tensor_scalar(
+                    out=dst, in0=src, scalar1=BF16_MAX, scalar2=0.0, op0=ALU.min, op1=ALU.max
+                )
+
+        def h_quant(g, r):
+            lo = g * B + 512 * r
+            nc.vector.quantize_mx(
+                out=hq[:, lo : lo + 512].bitcast(FP8X4),
+                scales=hs[:, lo : lo + 512],
+                in_=hg[:, 4 * lo : 4 * lo + 2048],
+            )
+
+        for jj in range(4):
+            for g in range(2):
+                z_bank(jj, g)
+        for jj, g in ((0, 0), (0, 1), (1, 0), (1, 1), (2, 0), (3, 0)):
+            stats(jj, g)
+        aggregate(0)
+        for j in range(5):
+            w_bank(j)
+        root(0)
+        stats(2, 1)
+        chain(0)
+        norm("g", 0, 1, range(4))
+        for j in range(5, NT):
+            w_bank(j)
+        stats(3, 1)
+        aggregate(1)
+        norm("s", 0, 0, (0, 1))
+        root(1)
+        norm("s", 0, 0, (2, 3))
+        w_quant(0)
+        chain(1)
+        regroup("g", 0, 1)
+        norm("s", 1, 0, range(4))
+        norm("g", 1, 1, range(4))
+        regroup("g", 1, 1)
+        regroup("v", 0, 0)
+        w_quant(1)
+        h_quant(0, 0)
+        regroup("v", 1, 0)
+        h_quant(1, 0)
+
+        logit = []
+        for j in range(NT):
+            lg = rows.tile([P, C], F32, name="lg")
+            logit.append(lg)
+            for n in range(2):
+                acc = psum.tile([P, 512], F32, tag="bank", name="acc")
+                for g in range(2):
+                    nc.tensor.matmul_mx(
+                        out=acc[:],
+                        lhsT=hq[:, g * B + P * j : g * B + P * j + P].bitcast(FP8X4),
+                        lhsT_scale=hs[:, g * B + P * j : g * B + P * j + P],
+                        rhs=wq[:, g * C + 512 * n : g * C + 512 * n + 512].bitcast(FP8X4),
+                        rhs_scale=ws[:, g * C + 512 * n : g * C + 512 * n + 512],
+                        start=(g == 0),
+                        stop=(g == 1),
+                    )
+                nc.vector.tensor_tensor(
+                    out=lg[:, 512 * n : 512 * n + 512], in0=acc[:], in1=bias[:, 512 * n : 512 * n + 512], op=ALU.add
+                )
+            nc.vector.tensor_reduce(out=negm[:, j : j + 1], in_=lg[:], axis=AX.X, op=ALU.max, negate=True)
+            ex = junk.tile([P, C], BF16, name="ex")
+            nc.scalar.activation(
+                out=ex[:], in_=lg[:], func=ACT.Exp, bias=negm[:, j : j + 1], scale=1.0,
+                accum_out=sums[:, j : j + 1],
+            )
+            if j == 1:
+                h_quant(0, 1)
+                h_quant(1, 1)
+            if j == 4 or j == 7:
+                first = 0 if j == 4 else 5
+                gs = slice(first, j + 1)
+                nc.scalar.activation(out=lns[:, gs], in_=sums[:, gs], func=ACT.Ln)
+                negc = negc_a if j == 4 else negc_b
+                if j == 4:
+                    nc.gpsimd.tensor_tensor(out=negc[:, gs], in0=negm[:, gs], in1=lns[:, gs], op=ALU.subtract)
+                    who = "ggggg"
+                else:
+                    nc.vector.tensor_tensor(out=negc[:, gs], in0=negm[:, gs], in1=lns[:, gs], op=ALU.subtract)
+                    who = "vsv"
+                for a in range(len(who)):
+                    i = first + a
+                    if who[a] == "g":
+                        nc.gpsimd.tensor_scalar(
+                            out=logit[i][:], in0=logit[i][:], scalar1=1.0, scalar2=negc[:, i : i + 1],
+                            op0=ALU.mult, op1=ALU.add,
+                        )
+                    elif who[a] == "v":
+                        nc.vector.tensor_scalar(
+                            out=logit[i][:], in0=logit[i][:], scalar1=negc[:, i : i + 1], scalar2=None, op0=ALU.add
+                        )
+                    else:
+                        nc.scalar.activation(
+                            out=logit[i][:], in_=logit[i][:], func=ACT.Identity, bias=negc[:, i : i + 1], scale=1.0
+                        )
+                    nc.sync.dma_start(out=out_view[i], in_=logit[i][:])

@@ -19,6 +19,7 @@ B = 1024
 K = 1024
 C = 1024
 NT = B // P
+NCH = 5
 BN_EPS = 1e-5
 BF16_MAX = 3.3895313892515355e38
 
@@ -28,7 +29,6 @@ def tile_binarymlp_pb_kernel(tc, z2, g2, beta2, W3, b3, out):
     with ExitStack() as ctx:
         ctx.enter_context(tc.manual_schedule())
         keep = ctx.enter_context(tc.tile_pool(name="keep", bufs=1))
-        rows = ctx.enter_context(tc.tile_pool(name="rows", bufs=NT))
         junk = ctx.enter_context(tc.tile_pool(name="junk", bufs=2))
         psum = ctx.enter_context(tc.psum_pool(name="psum", bufs=8))
 
@@ -41,31 +41,16 @@ def tile_binarymlp_pb_kernel(tc, z2, g2, beta2, W3, b3, out):
 
         z_nat = keep.tile([P, NT, K], BF16, name="z_nat")
         z_view = z2.rearrange("(p t) f -> p t f", t=NT)
-        for c in range(4):
-            nc.sync.dma_start(out=z_nat[:, 2 * c : 2 * c + 2, :], in_=z_view[:, 2 * c : 2 * c + 2, :])
         gamma = keep.tile([P, 8], BF16, name="gamma")
         beta = keep.tile([P, 8], BF16, name="beta")
-        with nc.allow_non_contiguous_dma(reason="two small vectors, a pair of features to a partition"):
-            nc.sync.dma_start(
-                out=gamma[:].rearrange("p (v e) -> p v e", e=2),
-                in_=g2.rearrange("(v q e) -> q v e", v=4, e=2),
-            )
-            nc.sync.dma_start(
-                out=beta[:].rearrange("p (v e) -> p v e", e=2),
-                in_=beta2.rearrange("(v q e) -> q v e", v=4, e=2),
-            )
         w_nat = keep.tile([P, NT, K], BF16, name="w_nat")
         w_view = W3.rearrange("(j p) f -> p j f", p=P)
-        for c in range(4):
-            nc.sync.dma_start(out=w_nat[:, 2 * c : 2 * c + 2, :], in_=w_view[:, 2 * c : 2 * c + 2, :])
         bias = keep.tile([P, C], BF16, name="bias")
-        nc.sync.dma_start(out=bias[:], in_=b3.partition_broadcast(P))
-
         zw = keep.tile([P, 4 * B], F32, name="zw")
         zw3 = zw[:].rearrange("p (v b) -> p v b", v=4)
         zwb = zw[:].bitcast(BF16)
         zw4 = zwb.rearrange("p (v b e) -> p v b e", v=4, e=2)
-        st = keep.tile([P, 4, 4, 6], F32, name="st")
+        st = keep.tile([P, 4, NCH, 6], F32, name="st")
         mv = keep.tile([P, 8, 2], F32, name="mv")
         vare = keep.tile([P, 8], F32, name="vare")
         std = keep.tile([P, 8], F32, name="std")
@@ -81,38 +66,57 @@ def tile_binarymlp_pb_kernel(tc, z2, g2, beta2, W3, b3, out):
         hg = keep.tile([P, 2 * B * 4], BF16, name="hg", align_bytes=64)
         hq = keep.tile([P, 2 * B], U32, name="hq", align_bytes=64)
         hs = keep.tile([P, 2 * B], U8, name="hs", align_bytes=64)
+        lg = keep.tile([P, NT, C], F32, name="lg")
         negm = keep.tile([P, NT], F32, name="negm")
         sums = keep.tile([P, NT], F32, name="sums")
-        lns = keep.tile([P, NT], F32, name="lns")
-        negc_a = keep.tile([P, NT], F32, name="negc_a")
-        negc_b = keep.tile([P, NT], F32, name="negc_b")
         out_view = out.rearrange("(p t) c -> t p c", t=NT)
+        acc = {}
+        shift = {}
 
-        def z_bank(jj, g):
-            zbank = psum.tile([P, 512], F32, tag="bank", name="zbank")
-            for u in range(2):
-                for jl in range(2):
-                    v = 2 * g + u
-                    nc.tensor.transpose(
-                        zbank[:, 256 * u + 128 * jl : 256 * u + 128 * jl + 128],
-                        z_nat[:, 2 * jj + jl, :].bitcast(F32)[:, 128 * v : 128 * v + 128],
-                        ident[:],
-                    )
-            nc.scalar.copy(
-                out=zw3[:, 2 * g : 2 * g + 2, 256 * jj : 256 * jj + 256],
-                in_=zbank[:].rearrange("p (u b) -> p u b", u=2),
+        def z_load(j0, nj, g0, ng):
+            nc.sync.dma_start(
+                out=z_nat[:, j0 : j0 + nj, 512 * g0 : 512 * (g0 + ng)],
+                in_=z_view[:, j0 : j0 + nj, 512 * g0 : 512 * (g0 + ng)],
             )
 
-        def stats(jj, g):
-            for u in range(2):
-                v = 2 * g + u
-                lo = 2 * (v * B + 256 * jj)
-                nc.vector.bn_stats(out=st[:, v, jj, :], in_=zwb[:, lo : lo + 512])
+        def gain_shift_load():
+            with nc.allow_non_contiguous_dma(reason="two small vectors, a pair of features to a partition"):
+                nc.sync.dma_start(
+                    out=gamma[:].rearrange("p (v e) -> p v e", e=2),
+                    in_=g2.rearrange("(v q e) -> q v e", v=4, e=2),
+                )
+                nc.sync.dma_start(
+                    out=beta[:].rearrange("p (v e) -> p v e", e=2),
+                    in_=beta2.rearrange("(v q e) -> q v e", v=4, e=2),
+                )
+
+        def w_load(j0, nj):
+            nc.sync.dma_start(out=w_nat[:, j0 : j0 + nj, :], in_=w_view[:, j0 : j0 + nj, :])
+
+        def bias_load():
+            nc.sync.dma_start(out=bias[:], in_=b3.partition_broadcast(P))
+
+        def z_bank(v0, nv, b0, nb):
+            zbank = psum.tile([P, 512], F32, tag="bank", name="zbank")
+            for v in range(v0, v0 + nv):
+                for j in range(b0 // P, (b0 + nb) // P):
+                    lo = (v - v0) * nb + P * j - b0
+                    nc.tensor.transpose(
+                        zbank[:, lo : lo + P], z_nat[:, j, :].bitcast(F32)[:, P * v : P * v + P], ident[:]
+                    )
+            nc.scalar.copy(
+                out=zw3[:, v0 : v0 + nv, b0 : b0 + nb],
+                in_=zbank[:, : nv * nb].rearrange("p (v b) -> p v b", v=nv),
+            )
+
+        def stats(v0, nv, b0, nb, piece):
+            for v in range(v0, v0 + nv):
+                lo = 2 * (v * B + b0)
+                nc.vector.bn_stats(out=st[:, v, piece, :], in_=zwb[:, lo : lo + 2 * nb])
 
         def aggregate(g):
-            for u in range(2):
+            for v in (2 * g, 2 * g + 1):
                 for e in range(2):
-                    v = 2 * g + u
                     nc.vector.bn_aggr(out=mv[:, 2 * v + e, :], in_=st[:, v, :, 3 * e : 3 * e + 3])
             cs = slice(4 * g, 4 * g + 4)
             nc.vector.tensor_scalar(out=vare[:, cs], in0=mv[:, cs, 1], scalar1=BN_EPS, scalar2=None, op0=ALU.add)
@@ -132,23 +136,18 @@ def tile_binarymlp_pb_kernel(tc, z2, g2, beta2, W3, b3, out):
             wbank = psum.tile([P, 512], F32, tag="bank", name="wbank")
             for v in range(4):
                 nc.tensor.transpose(
-                    wbank[:, 128 * v : 128 * v + 128],
-                    w_nat[:, j, :].bitcast(F32)[:, 128 * v : 128 * v + 128],
-                    ident[:],
+                    wbank[:, P * v : P * v + P], w_nat[:, j, :].bitcast(F32)[:, P * v : P * v + P], ident[:]
                 )
             nc.scalar.copy(
-                out=wg_words[:, :, 128 * j : 128 * j + 128, :],
+                out=wg_words[:, :, P * j : P * j + P, :],
                 in_=wbank[:].rearrange("p (g u c) -> p g c u", g=2, u=2),
             )
 
-        def w_quant(n):
-            for g in range(2):
-                lo = g * C + 512 * n
-                nc.vector.quantize_mx(
-                    out=wq[:, lo : lo + 512].bitcast(FP8X4),
-                    scales=ws[:, lo : lo + 512],
-                    in_=wg[:, 4 * lo : 4 * lo + 2048],
-                )
+        def w_quant(n, g):
+            lo = g * C + 512 * n
+            nc.vector.quantize_mx(
+                out=wq[:, lo : lo + 512].bitcast(FP8X4), scales=ws[:, lo : lo + 512], in_=wg[:, 4 * lo : 4 * lo + 2048]
+            )
 
         def norm(engine, g, r, ts):
             bs = slice(512 * r, 512 * r + 512)
@@ -158,6 +157,11 @@ def tile_binarymlp_pb_kernel(tc, z2, g2, beta2, W3, b3, out):
                 if engine == "s":
                     nc.scalar.activation(
                         out=hT[:, c, bs], in_=src, func=ACT.Relu, bias=bi[:, c : c + 1], scale=sc[:, c : c + 1]
+                    )
+                elif engine == "v":
+                    nc.vector.tensor_scalar(
+                        out=hT[:, c, bs], in0=src, scalar1=sc[:, c : c + 1], scalar2=bi[:, c : c + 1],
+                        op0=ALU.mult, op1=ALU.add,
                     )
                 else:
                     nc.gpsimd.tensor_scalar(
@@ -171,102 +175,182 @@ def tile_binarymlp_pb_kernel(tc, z2, g2, beta2, W3, b3, out):
             src = hT[:, 4 * g : 4 * g + 4, 512 * r : 512 * r + 512].rearrange("p t (c i) -> p c t i", i=4)
             if engine == "v":
                 nc.vector.tensor_scalar(out=dst, in0=src, scalar1=0.0, scalar2=None, op0=ALU.max)
+            elif engine == "s":
+                nc.scalar.activation(out=dst, in_=src, func=ACT.Relu)
             else:
-                nc.gpsimd.tensor_scalar(
-                    out=dst, in0=src, scalar1=BF16_MAX, scalar2=0.0, op0=ALU.min, op1=ALU.max
-                )
+                nc.gpsimd.tensor_scalar(out=dst, in0=src, scalar1=BF16_MAX, scalar2=0.0, op0=ALU.min, op1=ALU.max)
 
         def h_quant(g, r):
             lo = g * B + 512 * r
             nc.vector.quantize_mx(
-                out=hq[:, lo : lo + 512].bitcast(FP8X4),
-                scales=hs[:, lo : lo + 512],
-                in_=hg[:, 4 * lo : 4 * lo + 2048],
+                out=hq[:, lo : lo + 512].bitcast(FP8X4), scales=hs[:, lo : lo + 512], in_=hg[:, 4 * lo : 4 * lo + 2048]
             )
 
-        for jj in range(4):
+        def logits(j, n):
+            bank = psum.tile([P, 512], F32, tag="bank", name="acc")
+            acc[(j, n)] = bank
             for g in range(2):
-                z_bank(jj, g)
-        for jj, g in ((0, 0), (0, 1), (1, 0), (1, 1), (2, 0), (3, 0)):
-            stats(jj, g)
-        aggregate(0)
-        for j in range(5):
-            w_bank(j)
-        root(0)
-        stats(2, 1)
-        chain(0)
-        norm("g", 0, 1, range(4))
-        for j in range(5, NT):
-            w_bank(j)
-        stats(3, 1)
-        aggregate(1)
-        norm("s", 0, 0, (0, 1))
-        root(1)
-        norm("s", 0, 0, (2, 3))
-        w_quant(0)
-        chain(1)
-        regroup("g", 0, 1)
-        norm("s", 1, 0, range(4))
-        norm("g", 1, 1, range(4))
-        regroup("g", 1, 1)
-        regroup("v", 0, 0)
-        w_quant(1)
-        h_quant(0, 0)
-        regroup("v", 1, 0)
-        h_quant(1, 0)
-
-        logit = []
-        for j in range(NT):
-            lg = rows.tile([P, C], F32, name="lg")
-            logit.append(lg)
-            for n in range(2):
-                acc = psum.tile([P, 512], F32, tag="bank", name="acc")
-                for g in range(2):
-                    nc.tensor.matmul_mx(
-                        out=acc[:],
-                        lhsT=hq[:, g * B + P * j : g * B + P * j + P].bitcast(FP8X4),
-                        lhsT_scale=hs[:, g * B + P * j : g * B + P * j + P],
-                        rhs=wq[:, g * C + 512 * n : g * C + 512 * n + 512].bitcast(FP8X4),
-                        rhs_scale=ws[:, g * C + 512 * n : g * C + 512 * n + 512],
-                        start=(g == 0),
-                        stop=(g == 1),
-                    )
-                nc.vector.tensor_tensor(
-                    out=lg[:, 512 * n : 512 * n + 512], in0=acc[:], in1=bias[:, 512 * n : 512 * n + 512], op=ALU.add
+                nc.tensor.matmul_mx(
+                    out=bank[:],
+                    lhsT=hq[:, g * B + P * j : g * B + P * j + P].bitcast(FP8X4),
+                    lhsT_scale=hs[:, g * B + P * j : g * B + P * j + P],
+                    rhs=wq[:, g * C + 512 * n : g * C + 512 * n + 512].bitcast(FP8X4),
+                    rhs_scale=ws[:, g * C + 512 * n : g * C + 512 * n + 512],
+                    start=(g == 0),
+                    stop=(g == 1),
                 )
-            nc.vector.tensor_reduce(out=negm[:, j : j + 1], in_=lg[:], axis=AX.X, op=ALU.max, negate=True)
+
+        def add_bias(j, n):
+            cols = slice(512 * n, 512 * n + 512)
+            nc.vector.tensor_tensor(out=lg[:, j, cols], in0=acc[(j, n)][:], in1=bias[:, cols], op=ALU.add)
+
+        def row_max(j):
+            nc.vector.tensor_reduce(out=negm[:, j : j + 1], in_=lg[:, j, :], axis=AX.X, op=ALU.max, negate=True)
+
+        def exp_sum(j):
             ex = junk.tile([P, C], BF16, name="ex")
             nc.scalar.activation(
-                out=ex[:], in_=lg[:], func=ACT.Exp, bias=negm[:, j : j + 1], scale=1.0,
+                out=ex[:], in_=lg[:, j, :], func=ACT.Exp, bias=negm[:, j : j + 1], scale=1.0,
                 accum_out=sums[:, j : j + 1],
             )
-            if j == 1:
-                h_quant(0, 1)
-                h_quant(1, 1)
-            if j == 4 or j == 7:
-                first = 0 if j == 4 else 5
-                gs = slice(first, j + 1)
-                nc.scalar.activation(out=lns[:, gs], in_=sums[:, gs], func=ACT.Ln)
-                negc = negc_a if j == 4 else negc_b
-                if j == 4:
-                    nc.gpsimd.tensor_tensor(out=negc[:, gs], in0=negm[:, gs], in1=lns[:, gs], op=ALU.subtract)
-                    who = "ggggg"
-                else:
-                    nc.vector.tensor_tensor(out=negc[:, gs], in0=negm[:, gs], in1=lns[:, gs], op=ALU.subtract)
-                    who = "vsv"
-                for a in range(len(who)):
-                    i = first + a
-                    if who[a] == "g":
-                        nc.gpsimd.tensor_scalar(
-                            out=logit[i][:], in0=logit[i][:], scalar1=1.0, scalar2=negc[:, i : i + 1],
-                            op0=ALU.mult, op1=ALU.add,
-                        )
-                    elif who[a] == "v":
-                        nc.vector.tensor_scalar(
-                            out=logit[i][:], in0=logit[i][:], scalar1=negc[:, i : i + 1], scalar2=None, op0=ALU.add
-                        )
-                    else:
-                        nc.scalar.activation(
-                            out=logit[i][:], in_=logit[i][:], func=ACT.Identity, bias=negc[:, i : i + 1], scale=1.0
-                        )
-                    nc.sync.dma_start(out=out_view[i], in_=logit[i][:])
+
+        def log_sum(engine, j0, j1):
+            lns = keep.tile([P, NT], F32, name="lns%d" % j0)
+            negc = keep.tile([P, NT], F32, name="negc%d" % j0)
+            nc.scalar.activation(out=lns[:, j0:j1], in_=sums[:, j0:j1], func=ACT.Ln)
+            eng = nc.vector if engine == "v" else nc.gpsimd
+            eng.tensor_tensor(out=negc[:, j0:j1], in0=negm[:, j0:j1], in1=lns[:, j0:j1], op=ALU.subtract)
+            for j in range(j0, j1):
+                shift[j] = negc[:, j : j + 1]
+
+        def finish(engine, j):
+            if engine == "v":
+                nc.vector.tensor_scalar(out=lg[:, j, :], in0=lg[:, j, :], scalar1=shift[j], scalar2=None, op0=ALU.add)
+            elif engine == "s":
+                nc.scalar.activation(out=lg[:, j, :], in_=lg[:, j, :], func=ACT.Identity, bias=shift[j], scale=1.0)
+            else:
+                nc.gpsimd.tensor_scalar(
+                    out=lg[:, j, :], in0=lg[:, j, :], scalar1=1.0, scalar2=shift[j], op0=ALU.mult, op1=ALU.add
+                )
+            nc.sync.dma_start(out=out_view[j], in_=lg[:, j, :])
+
+        z_load(0, 1, 0, 1)
+        z_load(0, 1, 1, 1)
+        z_load(1, 1, 0, 2)
+        z_load(2, 2, 0, 2)
+        z_load(4, 2, 0, 2)
+        z_load(6, 2, 0, 2)
+        gain_shift_load()
+        w_load(0, 2)
+        w_load(2, 2)
+        w_load(4, 2)
+        w_load(6, 2)
+        bias_load()
+        z_bank(0, 2, 0, 128)
+        z_bank(2, 2, 0, 128)
+        z_bank(0, 4, 128, 128)
+        z_bank(0, 2, 256, 256)
+        z_bank(2, 2, 256, 256)
+        z_bank(0, 2, 512, 256)
+        z_bank(2, 2, 512, 256)
+        z_bank(0, 2, 768, 256)
+        z_bank(2, 2, 768, 256)
+        stats(0, 2, 0, 128, 0)
+        stats(2, 2, 0, 128, 0)
+        stats(0, 4, 128, 128, 1)
+        stats(0, 2, 256, 256, 2)
+        stats(2, 2, 256, 256, 2)
+        stats(0, 2, 512, 256, 3)
+        stats(0, 2, 768, 256, 4)
+        aggregate(0)
+        w_bank(0)
+        w_bank(1)
+        w_bank(2)
+        w_bank(3)
+        root(0)
+        stats(2, 2, 512, 256, 3)
+        chain(0)
+        w_bank(4)
+        stats(2, 2, 768, 256, 4)
+        aggregate(1)
+        norm("s", 0, 0, (0, 1, 2,))
+        root(1)
+        norm("s", 0, 0, (3,))
+        w_quant(0, 0)
+        w_quant(0, 1)
+        chain(1)
+        norm("v", 1, 0, (2, 3,))
+        norm("s", 1, 0, (0, 1,))
+        w_bank(5)
+        w_bank(6)
+        w_bank(7)
+        regroup("v", 0, 0)
+        regroup("v", 1, 0)
+        h_quant(0, 0)
+        h_quant(1, 0)
+        w_quant(1, 0)
+        w_quant(1, 1)
+        norm("s", 0, 1, (0, 1, 2, 3,))
+        norm("s", 1, 1, (0, 1, 2, 3,))
+        regroup("s", 0, 1)
+        regroup("s", 1, 1)
+        logits(0, 0)
+        add_bias(0, 0)
+        logits(0, 1)
+        add_bias(0, 1)
+        row_max(0)
+        logits(1, 0)
+        add_bias(1, 0)
+        logits(1, 1)
+        add_bias(1, 1)
+        row_max(1)
+        logits(2, 0)
+        add_bias(2, 0)
+        logits(2, 1)
+        add_bias(2, 1)
+        row_max(2)
+        h_quant(0, 1)
+        h_quant(1, 1)
+        exp_sum(0)
+        exp_sum(1)
+        exp_sum(2)
+        logits(3, 0)
+        add_bias(3, 0)
+        logits(3, 1)
+        add_bias(3, 1)
+        row_max(3)
+        exp_sum(3)
+        logits(4, 0)
+        add_bias(4, 0)
+        logits(4, 1)
+        add_bias(4, 1)
+        row_max(4)
+        exp_sum(4)
+        log_sum("g", 0, 5)
+        logits(5, 0)
+        add_bias(5, 0)
+        logits(5, 1)
+        add_bias(5, 1)
+        row_max(5)
+        exp_sum(5)
+        logits(6, 0)
+        add_bias(6, 0)
+        logits(6, 1)
+        add_bias(6, 1)
+        row_max(6)
+        exp_sum(6)
+        finish("v", 0)
+        finish("v", 1)
+        finish("v", 2)
+        logits(7, 0)
+        add_bias(7, 0)
+        logits(7, 1)
+        add_bias(7, 1)
+        row_max(7)
+        exp_sum(7)
+        finish("v", 3)
+        finish("v", 4)
+        log_sum("v", 5, 8)
+        finish("v", 5)
+        finish("s", 6)
+        finish("v", 7)

@@ -19,16 +19,14 @@ B = 1024
 K = 1024
 C = 1024
 NT = B // P
-NCH = 5
 BN_EPS = 1e-5
-BF16_MAX = 3.3895313892515355e38
 
 
 def tile_binarymlp_pb_kernel(tc, z2, g2, beta2, W3, b3, out):
     nc = tc.nc
     with ExitStack() as ctx:
-        ctx.enter_context(tc.manual_schedule())
         keep = ctx.enter_context(tc.tile_pool(name="keep", bufs=1))
+        rows = ctx.enter_context(tc.tile_pool(name="rows", bufs=NT))
         junk = ctx.enter_context(tc.tile_pool(name="junk", bufs=2))
         psum = ctx.enter_context(tc.psum_pool(name="psum", bufs=8))
 
@@ -41,16 +39,61 @@ def tile_binarymlp_pb_kernel(tc, z2, g2, beta2, W3, b3, out):
 
         z_nat = keep.tile([P, NT, K], BF16, name="z_nat")
         z_view = z2.rearrange("(p t) f -> p t f", t=NT)
+        for c in range(4):
+            nc.sync.dma_start(out=z_nat[:, 2 * c : 2 * c + 2, :], in_=z_view[:, 2 * c : 2 * c + 2, :])
         gamma = keep.tile([P, 8], BF16, name="gamma")
         beta = keep.tile([P, 8], BF16, name="beta")
+        with nc.allow_non_contiguous_dma(reason="two small vectors, a pair of features to a partition"):
+            nc.sync.dma_start(
+                out=gamma[:].rearrange("p (v e) -> p v e", e=2),
+                in_=g2.rearrange("(v q e) -> q v e", v=4, e=2),
+            )
+            nc.sync.dma_start(
+                out=beta[:].rearrange("p (v e) -> p v e", e=2),
+                in_=beta2.rearrange("(v q e) -> q v e", v=4, e=2),
+            )
         w_nat = keep.tile([P, NT, K], BF16, name="w_nat")
         w_view = W3.rearrange("(j p) f -> p j f", p=P)
+        for c in range(4):
+            nc.sync.dma_start(out=w_nat[:, 2 * c : 2 * c + 2, :], in_=w_view[:, 2 * c : 2 * c + 2, :])
         bias = keep.tile([P, C], BF16, name="bias")
-        zw = keep.tile([P, 4 * B], F32, name="zw")
-        zw3 = zw[:].rearrange("p (v b) -> p v b", v=4)
-        zwb = zw[:].bitcast(BF16)
-        zw4 = zwb.rearrange("p (v b e) -> p v b e", v=4, e=2)
-        st = keep.tile([P, 4, NCH, 6], F32, name="st")
+        nc.sync.dma_start(out=bias[:], in_=b3.partition_broadcast(P))
+
+        zT = keep.tile([P, 8, B], BF16, name="zT")
+        st = keep.tile([P, 8, 4, 6], F32, name="st")
+        for jj in range(4):
+            for g in range(2):
+                zbank = psum.tile([P, 512], F32, tag="bank", name="zbank")
+                for u in range(2):
+                    for jl in range(2):
+                        v = 2 * g + u
+                        nc.tensor.transpose(
+                            zbank[:, 256 * u + 128 * jl : 256 * u + 128 * jl + 128],
+                            z_nat[:, 2 * jj + jl, :].bitcast(F32)[:, 128 * v : 128 * v + 128],
+                            ident[:],
+                        )
+                nc.scalar.copy(
+                    out=zT[:, 4 * g : 4 * g + 4, 256 * jj : 256 * jj + 256].rearrange("p (u e) b -> p u e b", e=2),
+                    in_=zbank[:].bitcast(BF16).rearrange("p (u b e) -> p u e b", u=2, e=2),
+                )
+                for t in range(4):
+                    nc.vector.bn_stats(out=st[:, 4 * g + t, jj, :], in_=zT[:, 4 * g + t, 256 * jj : 256 * jj + 256])
+
+        wg = keep.tile([P, 2 * C * 4], BF16, name="wg", align_bytes=64)
+        wg_words = wg[:].bitcast(F32).rearrange("p (g c u) -> p g c u", g=2, u=2)
+        for j in range(NT):
+            wbank = psum.tile([P, 512], F32, tag="bank", name="wbank")
+            for v in range(4):
+                nc.tensor.transpose(
+                    wbank[:, 128 * v : 128 * v + 128],
+                    w_nat[:, j, :].bitcast(F32)[:, 128 * v : 128 * v + 128],
+                    ident[:],
+                )
+            nc.scalar.copy(
+                out=wg_words[:, :, 128 * j : 128 * j + 128, :],
+                in_=wbank[:].rearrange("p (g u c) -> p g c u", g=2, u=2),
+            )
+
         mv = keep.tile([P, 8, 2], F32, name="mv")
         vare = keep.tile([P, 8], F32, name="vare")
         std = keep.tile([P, 8], F32, name="std")
@@ -58,299 +101,111 @@ def tile_binarymlp_pb_kernel(tc, z2, g2, beta2, W3, b3, out):
         sc = keep.tile([P, 8], F32, name="sc")
         msc = keep.tile([P, 8], F32, name="msc")
         bi = keep.tile([P, 8], F32, name="bi")
-        wg = keep.tile([P, 2 * C * 4], BF16, name="wg", align_bytes=64)
-        wg_words = wg[:].bitcast(F32).rearrange("p (g c u) -> p g c u", g=2, u=2)
-        wq = keep.tile([P, 2 * C], U32, name="wq", align_bytes=64)
-        ws = keep.tile([P, 2 * C], U8, name="ws", align_bytes=64)
-        hT = keep.tile([P, 8, B], BF16, name="hT")
-        hg = keep.tile([P, 2 * B * 4], BF16, name="hg", align_bytes=64)
-        hq = keep.tile([P, 2 * B], U32, name="hq", align_bytes=64)
-        hs = keep.tile([P, 2 * B], U8, name="hs", align_bytes=64)
-        lg = keep.tile([P, NT, C], F32, name="lg")
-        negm = keep.tile([P, NT], F32, name="negm")
-        sums = keep.tile([P, NT], F32, name="sums")
-        out_view = out.rearrange("(p t) c -> t p c", t=NT)
-        acc = {}
-        shift = {}
-
-        def z_load(j0, nj, g0, ng):
-            nc.sync.dma_start(
-                out=z_nat[:, j0 : j0 + nj, 512 * g0 : 512 * (g0 + ng)],
-                in_=z_view[:, j0 : j0 + nj, 512 * g0 : 512 * (g0 + ng)],
-            )
-
-        def gain_shift_load():
-            with nc.allow_non_contiguous_dma(reason="two small vectors, a pair of features to a partition"):
-                nc.sync.dma_start(
-                    out=gamma[:].rearrange("p (v e) -> p v e", e=2),
-                    in_=g2.rearrange("(v q e) -> q v e", v=4, e=2),
-                )
-                nc.sync.dma_start(
-                    out=beta[:].rearrange("p (v e) -> p v e", e=2),
-                    in_=beta2.rearrange("(v q e) -> q v e", v=4, e=2),
-                )
-
-        def w_load(j0, nj):
-            nc.sync.dma_start(out=w_nat[:, j0 : j0 + nj, :], in_=w_view[:, j0 : j0 + nj, :])
-
-        def bias_load():
-            nc.sync.dma_start(out=bias[:], in_=b3.partition_broadcast(P))
-
-        def z_bank(v0, nv, b0, nb):
-            zbank = psum.tile([P, 512], F32, tag="bank", name="zbank")
-            for v in range(v0, v0 + nv):
-                for j in range(b0 // P, (b0 + nb) // P):
-                    lo = (v - v0) * nb + P * j - b0
-                    nc.tensor.transpose(
-                        zbank[:, lo : lo + P], z_nat[:, j, :].bitcast(F32)[:, P * v : P * v + P], ident[:]
-                    )
-            nc.scalar.copy(
-                out=zw3[:, v0 : v0 + nv, b0 : b0 + nb],
-                in_=zbank[:, : nv * nb].rearrange("p (v b) -> p v b", v=nv),
-            )
-
-        def stats(v0, nv, b0, nb, piece):
-            for v in range(v0, v0 + nv):
-                lo = 2 * (v * B + b0)
-                nc.vector.bn_stats(out=st[:, v, piece, :], in_=zwb[:, lo : lo + 2 * nb])
-
-        def aggregate(g):
-            for v in (2 * g, 2 * g + 1):
-                for e in range(2):
-                    nc.vector.bn_aggr(out=mv[:, 2 * v + e, :], in_=st[:, v, :, 3 * e : 3 * e + 3])
+        for g in range(2):
             cs = slice(4 * g, 4 * g + 4)
+            for t in range(4):
+                nc.vector.bn_aggr(out=mv[:, 4 * g + t, :], in_=st[:, 4 * g + t, :, :].rearrange("p a s -> p (a s)"))
             nc.vector.tensor_scalar(out=vare[:, cs], in0=mv[:, cs, 1], scalar1=BN_EPS, scalar2=None, op0=ALU.add)
-
-        def root(g):
-            cs = slice(4 * g, 4 * g + 4)
             nc.scalar.activation(out=std[:, cs], in_=vare[:, cs], func=ACT.Sqrt)
-
-        def chain(g):
-            cs = slice(4 * g, 4 * g + 4)
             nc.vector.reciprocal(out=rstd[:, cs], in_=std[:, cs])
             nc.vector.tensor_tensor(out=sc[:, cs], in0=gamma[:, cs], in1=rstd[:, cs], op=ALU.mult)
             nc.vector.tensor_tensor(out=msc[:, cs], in0=mv[:, cs, 0], in1=sc[:, cs], op=ALU.mult)
             nc.vector.tensor_tensor(out=bi[:, cs], in0=beta[:, cs], in1=msc[:, cs], op=ALU.subtract)
 
-        def w_bank(j):
-            wbank = psum.tile([P, 512], F32, tag="bank", name="wbank")
-            for v in range(4):
-                nc.tensor.transpose(
-                    wbank[:, P * v : P * v + P], w_nat[:, j, :].bitcast(F32)[:, P * v : P * v + P], ident[:]
-                )
-            nc.scalar.copy(
-                out=wg_words[:, :, P * j : P * j + P, :],
-                in_=wbank[:].rearrange("p (g u c) -> p g c u", g=2, u=2),
-            )
-
-        def w_quant(n, g):
-            lo = g * C + 512 * n
-            nc.vector.quantize_mx(
-                out=wq[:, lo : lo + 512].bitcast(FP8X4), scales=ws[:, lo : lo + 512], in_=wg[:, 4 * lo : 4 * lo + 2048]
-            )
-
-        def norm(engine, g, r, ts):
-            bs = slice(512 * r, 512 * r + 512)
-            for t in ts:
-                c = 4 * g + t
-                src = zw4[:, c // 2, bs, c % 2]
-                if engine == "s":
-                    nc.scalar.activation(
-                        out=hT[:, c, bs], in_=src, func=ACT.Relu, bias=bi[:, c : c + 1], scale=sc[:, c : c + 1]
-                    )
-                elif engine == "v":
-                    nc.vector.tensor_scalar(
-                        out=hT[:, c, bs], in0=src, scalar1=sc[:, c : c + 1], scalar2=bi[:, c : c + 1],
-                        op0=ALU.mult, op1=ALU.add,
-                    )
-                else:
-                    nc.gpsimd.tensor_scalar(
-                        out=hT[:, c, bs], in0=src, scalar1=sc[:, c : c + 1], scalar2=bi[:, c : c + 1],
-                        op0=ALU.mult, op1=ALU.add,
-                    )
-
-        def regroup(engine, g, r):
-            lo = g * B + 512 * r
-            dst = hg[:, 4 * lo : 4 * lo + 2048].rearrange("p (c i t) -> p c t i", i=4, t=4)
-            src = hT[:, 4 * g : 4 * g + 4, 512 * r : 512 * r + 512].rearrange("p t (c i) -> p c t i", i=4)
-            if engine == "v":
-                nc.vector.tensor_scalar(out=dst, in0=src, scalar1=0.0, scalar2=None, op0=ALU.max)
-            elif engine == "s":
-                nc.scalar.activation(out=dst, in_=src, func=ACT.Relu)
-            else:
-                nc.gpsimd.tensor_scalar(out=dst, in0=src, scalar1=BF16_MAX, scalar2=0.0, op0=ALU.min, op1=ALU.max)
-
-        def h_quant(g, r):
-            lo = g * B + 512 * r
-            nc.vector.quantize_mx(
-                out=hq[:, lo : lo + 512].bitcast(FP8X4), scales=hs[:, lo : lo + 512], in_=hg[:, 4 * lo : 4 * lo + 2048]
-            )
-
-        def logits(j, n):
-            bank = psum.tile([P, 512], F32, tag="bank", name="acc")
-            acc[(j, n)] = bank
+        wq = keep.tile([P, 2 * C], U32, name="wq", align_bytes=64)
+        ws = keep.tile([P, 2 * C], U8, name="ws", align_bytes=64)
+        for n in range(2):
             for g in range(2):
-                nc.tensor.matmul_mx(
-                    out=bank[:],
-                    lhsT=hq[:, g * B + P * j : g * B + P * j + P].bitcast(FP8X4),
-                    lhsT_scale=hs[:, g * B + P * j : g * B + P * j + P],
-                    rhs=wq[:, g * C + 512 * n : g * C + 512 * n + 512].bitcast(FP8X4),
-                    rhs_scale=ws[:, g * C + 512 * n : g * C + 512 * n + 512],
-                    start=(g == 0),
-                    stop=(g == 1),
+                lo = g * C + 512 * n
+                nc.vector.quantize_mx(
+                    out=wq[:, lo : lo + 512].bitcast(FP8X4),
+                    scales=ws[:, lo : lo + 512],
+                    in_=wg[:, 4 * lo : 4 * lo + 2048],
                 )
 
-        def add_bias(j, n):
-            cols = slice(512 * n, 512 * n + 512)
-            nc.vector.tensor_tensor(out=lg[:, j, cols], in0=acc[(j, n)][:], in1=bias[:, cols], op=ALU.add)
+        hT = keep.tile([P, 8, B], BF16, name="hT")
+        hg = keep.tile([P, 2 * B * 4], BF16, name="hg", align_bytes=64)
+        hq = keep.tile([P, 2 * B], U32, name="hq", align_bytes=64)
+        hs = keep.tile([P, 2 * B], U8, name="hs", align_bytes=64)
+        for r in range(2):
+            for g in range(2):
+                bs = slice(512 * r, 512 * r + 512)
+                for t in range(4):
+                    c = 4 * g + t
+                    nc.vector.tensor_scalar(
+                        out=hT[:, c, bs], in0=zT[:, c, bs],
+                        scalar1=sc[:, c : c + 1], scalar2=bi[:, c : c + 1],
+                        op0=ALU.mult, op1=ALU.add,
+                    )
+                lo = g * B + 512 * r
+                dst = hg[:, 4 * lo : 4 * lo + 2048].rearrange("p (c i t) -> p c t i", i=4, t=4)
+                src = hT[:, 4 * g : 4 * g + 4, bs].rearrange("p t (c i) -> p c t i", i=4)
+                if r == 0:
+                    nc.vector.tensor_scalar(out=dst, in0=src, scalar1=0.0, scalar2=None, op0=ALU.max)
+                else:
+                    nc.scalar.activation(out=dst, in_=src, func=ACT.Relu)
+            for g in range(2):
+                lo = g * B + 512 * r
+                nc.vector.quantize_mx(
+                    out=hq[:, lo : lo + 512].bitcast(FP8X4),
+                    scales=hs[:, lo : lo + 512],
+                    in_=hg[:, 4 * lo : 4 * lo + 2048],
+                )
 
-        def row_max(j):
-            nc.vector.tensor_reduce(out=negm[:, j : j + 1], in_=lg[:, j, :], axis=AX.X, op=ALU.max, negate=True)
-
-        def exp_sum(j):
+        negm = keep.tile([P, NT], F32, name="negm")
+        sums = keep.tile([P, NT], F32, name="sums")
+        lns = keep.tile([P, NT], F32, name="lns")
+        negc_a = keep.tile([P, NT], F32, name="negc_a")
+        negc_b = keep.tile([P, NT], F32, name="negc_b")
+        out_view = out.rearrange("(p t) c -> t p c", t=NT)
+        logit = []
+        for j in range(NT):
+            lg = rows.tile([P, C], F32, name="lg")
+            logit.append(lg)
+            for n in range(2):
+                acc = psum.tile([P, 512], F32, tag="bank", name="acc")
+                for g in range(2):
+                    nc.tensor.matmul_mx(
+                        out=acc[:],
+                        lhsT=hq[:, g * B + P * j : g * B + P * j + P].bitcast(FP8X4),
+                        lhsT_scale=hs[:, g * B + P * j : g * B + P * j + P],
+                        rhs=wq[:, g * C + 512 * n : g * C + 512 * n + 512].bitcast(FP8X4),
+                        rhs_scale=ws[:, g * C + 512 * n : g * C + 512 * n + 512],
+                        start=(g == 0),
+                        stop=(g == 1),
+                    )
+                nc.vector.tensor_tensor(
+                    out=lg[:, 512 * n : 512 * n + 512], in0=acc[:], in1=bias[:, 512 * n : 512 * n + 512], op=ALU.add
+                )
+            nc.vector.tensor_reduce(out=negm[:, j : j + 1], in_=lg[:], axis=AX.X, op=ALU.max, negate=True)
             ex = junk.tile([P, C], BF16, name="ex")
             nc.scalar.activation(
-                out=ex[:], in_=lg[:, j, :], func=ACT.Exp, bias=negm[:, j : j + 1], scale=1.0,
+                out=ex[:], in_=lg[:], func=ACT.Exp, bias=negm[:, j : j + 1], scale=1.0,
                 accum_out=sums[:, j : j + 1],
             )
-
-        def log_sum(engine, j0, j1):
-            lns = keep.tile([P, NT], F32, name="lns%d" % j0)
-            negc = keep.tile([P, NT], F32, name="negc%d" % j0)
-            nc.scalar.activation(out=lns[:, j0:j1], in_=sums[:, j0:j1], func=ACT.Ln)
-            eng = nc.vector if engine == "v" else nc.gpsimd
-            eng.tensor_tensor(out=negc[:, j0:j1], in0=negm[:, j0:j1], in1=lns[:, j0:j1], op=ALU.subtract)
-            for j in range(j0, j1):
-                shift[j] = negc[:, j : j + 1]
-
-        def finish(engine, j):
-            if engine == "v":
-                nc.vector.tensor_scalar(out=lg[:, j, :], in0=lg[:, j, :], scalar1=shift[j], scalar2=None, op0=ALU.add)
-            elif engine == "s":
-                nc.scalar.activation(out=lg[:, j, :], in_=lg[:, j, :], func=ACT.Identity, bias=shift[j], scale=1.0)
-            else:
-                nc.gpsimd.tensor_scalar(
-                    out=lg[:, j, :], in0=lg[:, j, :], scalar1=1.0, scalar2=shift[j], op0=ALU.mult, op1=ALU.add
-                )
-            nc.sync.dma_start(out=out_view[j], in_=lg[:, j, :])
-
-        z_load(0, 1, 0, 1)
-        z_load(0, 1, 1, 1)
-        z_load(1, 1, 0, 2)
-        z_load(2, 2, 0, 2)
-        z_load(4, 2, 0, 2)
-        z_load(6, 2, 0, 2)
-        gain_shift_load()
-        w_load(0, 2)
-        w_load(2, 2)
-        w_load(4, 2)
-        w_load(6, 2)
-        bias_load()
-        z_bank(0, 2, 0, 128)
-        z_bank(2, 2, 0, 128)
-        z_bank(0, 4, 128, 128)
-        z_bank(0, 2, 256, 256)
-        z_bank(2, 2, 256, 256)
-        z_bank(0, 2, 512, 256)
-        z_bank(2, 2, 512, 256)
-        z_bank(0, 2, 768, 256)
-        z_bank(2, 2, 768, 256)
-        stats(0, 2, 0, 128, 0)
-        stats(2, 2, 0, 128, 0)
-        stats(0, 4, 128, 128, 1)
-        stats(0, 2, 256, 256, 2)
-        stats(2, 2, 256, 256, 2)
-        stats(0, 2, 512, 256, 3)
-        stats(0, 2, 768, 256, 4)
-        aggregate(0)
-        w_bank(0)
-        w_bank(1)
-        w_bank(2)
-        w_bank(3)
-        root(0)
-        stats(2, 2, 512, 256, 3)
-        chain(0)
-        w_bank(4)
-        stats(2, 2, 768, 256, 4)
-        aggregate(1)
-        norm("s", 0, 0, (0, 1, 2,))
-        root(1)
-        norm("s", 0, 0, (3,))
-        w_quant(0, 0)
-        w_quant(0, 1)
-        chain(1)
-        norm("v", 1, 0, (2, 3,))
-        norm("s", 1, 0, (0, 1,))
-        w_bank(5)
-        w_bank(6)
-        w_bank(7)
-        regroup("v", 0, 0)
-        regroup("v", 1, 0)
-        h_quant(0, 0)
-        h_quant(1, 0)
-        w_quant(1, 0)
-        w_quant(1, 1)
-        norm("s", 0, 1, (0, 1, 2, 3,))
-        norm("s", 1, 1, (0, 1, 2, 3,))
-        regroup("s", 0, 1)
-        regroup("s", 1, 1)
-        logits(0, 0)
-        add_bias(0, 0)
-        logits(0, 1)
-        add_bias(0, 1)
-        row_max(0)
-        logits(1, 0)
-        add_bias(1, 0)
-        logits(1, 1)
-        add_bias(1, 1)
-        row_max(1)
-        logits(2, 0)
-        add_bias(2, 0)
-        logits(2, 1)
-        add_bias(2, 1)
-        row_max(2)
-        h_quant(0, 1)
-        h_quant(1, 1)
-        exp_sum(0)
-        exp_sum(1)
-        exp_sum(2)
-        logits(3, 0)
-        add_bias(3, 0)
-        logits(3, 1)
-        add_bias(3, 1)
-        row_max(3)
-        exp_sum(3)
-        logits(4, 0)
-        add_bias(4, 0)
-        logits(4, 1)
-        add_bias(4, 1)
-        row_max(4)
-        exp_sum(4)
-        log_sum("g", 0, 5)
-        logits(5, 0)
-        add_bias(5, 0)
-        logits(5, 1)
-        add_bias(5, 1)
-        row_max(5)
-        exp_sum(5)
-        logits(6, 0)
-        add_bias(6, 0)
-        logits(6, 1)
-        add_bias(6, 1)
-        row_max(6)
-        exp_sum(6)
-        finish("v", 0)
-        finish("v", 1)
-        finish("v", 2)
-        logits(7, 0)
-        add_bias(7, 0)
-        logits(7, 1)
-        add_bias(7, 1)
-        row_max(7)
-        exp_sum(7)
-        finish("v", 3)
-        finish("v", 4)
-        log_sum("v", 5, 8)
-        finish("v", 5)
-        finish("s", 6)
-        finish("v", 7)
+            if j % 4 == 3:
+                gs = slice(j - 3, j + 1)
+                nc.scalar.activation(out=lns[:, gs], in_=sums[:, gs], func=ACT.Ln)
+                negc = negc_a if j == 3 else negc_b
+                if j == 3:
+                    nc.gpsimd.tensor_tensor(out=negc[:, gs], in0=negm[:, gs], in1=lns[:, gs], op=ALU.subtract)
+                    who = ["g", "g", "g", "g"]
+                else:
+                    nc.vector.tensor_tensor(out=negc[:, gs], in0=negm[:, gs], in1=lns[:, gs], op=ALU.subtract)
+                    who = ["v", "s", "g", "v"]
+                for a in range(4):
+                    i = j - 3 + a
+                    if who[a] == "g":
+                        nc.gpsimd.tensor_scalar(
+                            out=logit[i][:], in0=logit[i][:], scalar1=1.0, scalar2=negc[:, i : i + 1],
+                            op0=ALU.mult, op1=ALU.add,
+                        )
+                    elif who[a] == "v":
+                        nc.vector.tensor_scalar(
+                            out=logit[i][:], in0=logit[i][:], scalar1=negc[:, i : i + 1], scalar2=None, op0=ALU.add
+                        )
+                    else:
+                        nc.scalar.activation(
+                            out=logit[i][:], in_=logit[i][:], func=ACT.Identity, bias=negc[:, i : i + 1], scale=1.0
+                        )
+                    nc.sync.dma_start(out=out_view[i], in_=logit[i][:])

@@ -20,13 +20,13 @@ K = 1024
 C = 1024
 NT = B // P
 BN_EPS = 1e-5
+FIRST_GROUP = 5
 
 
 def tile_binarymlp_pb_kernel(tc, z2, g2, beta2, W3, b3, out):
     nc = tc.nc
     with ExitStack() as ctx:
         keep = ctx.enter_context(tc.tile_pool(name="keep", bufs=1))
-        rows = ctx.enter_context(tc.tile_pool(name="rows", bufs=NT))
         junk = ctx.enter_context(tc.tile_pool(name="junk", bufs=2))
         psum = ctx.enter_context(tc.psum_pool(name="psum", bufs=8))
 
@@ -39,18 +39,18 @@ def tile_binarymlp_pb_kernel(tc, z2, g2, beta2, W3, b3, out):
 
         z_nat = keep.tile([P, NT, K], BF16, name="z_nat")
         z_view = z2.rearrange("(p t) f -> p t f", t=NT)
-        for c in range(4):
+        for g in range(2):
+            nc.sync.dma_start(out=z_nat[:, 0:2, 512 * g : 512 * g + 512], in_=z_view[:, 0:2, 512 * g : 512 * g + 512])
+        for c in range(1, 4):
             nc.sync.dma_start(out=z_nat[:, 2 * c : 2 * c + 2, :], in_=z_view[:, 2 * c : 2 * c + 2, :])
         gamma = keep.tile([P, 8], BF16, name="gamma")
         beta = keep.tile([P, 8], BF16, name="beta")
         with nc.allow_non_contiguous_dma(reason="two small vectors, a pair of features to a partition"):
             nc.sync.dma_start(
-                out=gamma[:].rearrange("p (v e) -> p v e", e=2),
-                in_=g2.rearrange("(v q e) -> q v e", v=4, e=2),
+                out=gamma[:].rearrange("p (v e) -> p v e", e=2), in_=g2.rearrange("(v q e) -> q v e", v=4, e=2)
             )
             nc.sync.dma_start(
-                out=beta[:].rearrange("p (v e) -> p v e", e=2),
-                in_=beta2.rearrange("(v q e) -> q v e", v=4, e=2),
+                out=beta[:].rearrange("p (v e) -> p v e", e=2), in_=beta2.rearrange("(v q e) -> q v e", v=4, e=2)
             )
         w_nat = keep.tile([P, NT, K], BF16, name="w_nat")
         w_view = W3.rearrange("(j p) f -> p j f", p=P)
@@ -59,8 +59,11 @@ def tile_binarymlp_pb_kernel(tc, z2, g2, beta2, W3, b3, out):
         bias = keep.tile([P, C], BF16, name="bias")
         nc.sync.dma_start(out=bias[:], in_=b3.partition_broadcast(P))
 
-        zT = keep.tile([P, 8, B], BF16, name="zT")
-        st = keep.tile([P, 8, 4, 6], F32, name="st")
+        zw = keep.tile([P, 4 * B], F32, name="zw")
+        zw3 = zw[:].rearrange("p (v b) -> p v b", v=4)
+        zwb = zw[:].bitcast(BF16)
+        zw4 = zwb.rearrange("p (v b e) -> p v b e", v=4, e=2)
+        st = keep.tile([P, 4, 4, 6], F32, name="st")
         for jj in range(4):
             for g in range(2):
                 zbank = psum.tile([P, 512], F32, tag="bank", name="zbank")
@@ -68,16 +71,17 @@ def tile_binarymlp_pb_kernel(tc, z2, g2, beta2, W3, b3, out):
                     for jl in range(2):
                         v = 2 * g + u
                         nc.tensor.transpose(
-                            zbank[:, 256 * u + 128 * jl : 256 * u + 128 * jl + 128],
-                            z_nat[:, 2 * jj + jl, :].bitcast(F32)[:, 128 * v : 128 * v + 128],
+                            zbank[:, 256 * u + P * jl : 256 * u + P * jl + P],
+                            z_nat[:, 2 * jj + jl, :].bitcast(F32)[:, P * v : P * v + P],
                             ident[:],
                         )
                 nc.scalar.copy(
-                    out=zT[:, 4 * g : 4 * g + 4, 256 * jj : 256 * jj + 256].rearrange("p (u e) b -> p u e b", e=2),
-                    in_=zbank[:].bitcast(BF16).rearrange("p (u b e) -> p u e b", u=2, e=2),
+                    out=zw3[:, 2 * g : 2 * g + 2, 256 * jj : 256 * jj + 256],
+                    in_=zbank[:].rearrange("p (u b) -> p u b", u=2),
                 )
-                for t in range(4):
-                    nc.vector.bn_stats(out=st[:, 4 * g + t, jj, :], in_=zT[:, 4 * g + t, 256 * jj : 256 * jj + 256])
+                for v in (2 * g, 2 * g + 1):
+                    lo = 2 * (v * B + 256 * jj)
+                    nc.vector.bn_stats(out=st[:, v, jj, :], in_=zwb[:, lo : lo + 512])
 
         wg = keep.tile([P, 2 * C * 4], BF16, name="wg", align_bytes=64)
         wg_words = wg[:].bitcast(F32).rearrange("p (g c u) -> p g c u", g=2, u=2)
@@ -85,13 +89,10 @@ def tile_binarymlp_pb_kernel(tc, z2, g2, beta2, W3, b3, out):
             wbank = psum.tile([P, 512], F32, tag="bank", name="wbank")
             for v in range(4):
                 nc.tensor.transpose(
-                    wbank[:, 128 * v : 128 * v + 128],
-                    w_nat[:, j, :].bitcast(F32)[:, 128 * v : 128 * v + 128],
-                    ident[:],
+                    wbank[:, P * v : P * v + P], w_nat[:, j, :].bitcast(F32)[:, P * v : P * v + P], ident[:]
                 )
             nc.scalar.copy(
-                out=wg_words[:, :, 128 * j : 128 * j + 128, :],
-                in_=wbank[:].rearrange("p (g u c) -> p g c u", g=2, u=2),
+                out=wg_words[:, :, P * j : P * j + P, :], in_=wbank[:].rearrange("p (g u c) -> p g c u", g=2, u=2)
             )
 
         mv = keep.tile([P, 8, 2], F32, name="mv")
@@ -103,8 +104,9 @@ def tile_binarymlp_pb_kernel(tc, z2, g2, beta2, W3, b3, out):
         bi = keep.tile([P, 8], F32, name="bi")
         for g in range(2):
             cs = slice(4 * g, 4 * g + 4)
-            for t in range(4):
-                nc.vector.bn_aggr(out=mv[:, 4 * g + t, :], in_=st[:, 4 * g + t, :, :].rearrange("p a s -> p (a s)"))
+            for v in (2 * g, 2 * g + 1):
+                for e in range(2):
+                    nc.vector.bn_aggr(out=mv[:, 2 * v + e, :], in_=st[:, v, :, 3 * e : 3 * e + 3])
             nc.vector.tensor_scalar(out=vare[:, cs], in0=mv[:, cs, 1], scalar1=BN_EPS, scalar2=None, op0=ALU.add)
             nc.scalar.activation(out=std[:, cs], in_=vare[:, cs], func=ACT.Sqrt)
             nc.vector.reciprocal(out=rstd[:, cs], in_=std[:, cs])
@@ -114,55 +116,47 @@ def tile_binarymlp_pb_kernel(tc, z2, g2, beta2, W3, b3, out):
 
         wq = keep.tile([P, 2 * C], U32, name="wq", align_bytes=64)
         ws = keep.tile([P, 2 * C], U8, name="ws", align_bytes=64)
-        for n in range(2):
-            for g in range(2):
-                lo = g * C + 512 * n
-                nc.vector.quantize_mx(
-                    out=wq[:, lo : lo + 512].bitcast(FP8X4),
-                    scales=ws[:, lo : lo + 512],
-                    in_=wg[:, 4 * lo : 4 * lo + 2048],
-                )
-
         hT = keep.tile([P, 8, B], BF16, name="hT")
         hg = keep.tile([P, 2 * B * 4], BF16, name="hg", align_bytes=64)
         hq = keep.tile([P, 2 * B], U32, name="hq", align_bytes=64)
         hs = keep.tile([P, 2 * B], U8, name="hs", align_bytes=64)
         for r in range(2):
+            bs = slice(512 * r, 512 * r + 512)
             for g in range(2):
-                bs = slice(512 * r, 512 * r + 512)
                 for t in range(4):
                     c = 4 * g + t
                     nc.vector.tensor_scalar(
-                        out=hT[:, c, bs], in0=zT[:, c, bs],
-                        scalar1=sc[:, c : c + 1], scalar2=bi[:, c : c + 1],
-                        op0=ALU.mult, op1=ALU.add,
+                        out=hT[:, c, bs], in0=zw4[:, c // 2, bs, c % 2],
+                        scalar1=sc[:, c : c + 1], scalar2=bi[:, c : c + 1], op0=ALU.mult, op1=ALU.add,
                     )
                 lo = g * B + 512 * r
                 dst = hg[:, 4 * lo : 4 * lo + 2048].rearrange("p (c i t) -> p c t i", i=4, t=4)
                 src = hT[:, 4 * g : 4 * g + 4, bs].rearrange("p t (c i) -> p c t i", i=4)
-                if r == 0:
+                if r == 0 and g == 1:
                     nc.vector.tensor_scalar(out=dst, in0=src, scalar1=0.0, scalar2=None, op0=ALU.max)
                 else:
                     nc.scalar.activation(out=dst, in_=src, func=ACT.Relu)
             for g in range(2):
+                lo = g * C + 512 * r
+                nc.vector.quantize_mx(
+                    out=wq[:, lo : lo + 512].bitcast(FP8X4), scales=ws[:, lo : lo + 512], in_=wg[:, 4 * lo : 4 * lo + 2048]
+                )
+            for g in range(2):
                 lo = g * B + 512 * r
                 nc.vector.quantize_mx(
-                    out=hq[:, lo : lo + 512].bitcast(FP8X4),
-                    scales=hs[:, lo : lo + 512],
-                    in_=hg[:, 4 * lo : 4 * lo + 2048],
+                    out=hq[:, lo : lo + 512].bitcast(FP8X4), scales=hs[:, lo : lo + 512], in_=hg[:, 4 * lo : 4 * lo + 2048]
                 )
 
+        lg = keep.tile([P, NT, C], F32, name="lg")
         negm = keep.tile([P, NT], F32, name="negm")
         sums = keep.tile([P, NT], F32, name="sums")
         lns = keep.tile([P, NT], F32, name="lns")
-        negc_a = keep.tile([P, NT], F32, name="negc_a")
-        negc_b = keep.tile([P, NT], F32, name="negc_b")
+        negc_first = keep.tile([P, NT], F32, name="negc_first")
+        negc_last = keep.tile([P, NT], F32, name="negc_last")
         out_view = out.rearrange("(p t) c -> t p c", t=NT)
-        logit = []
         for j in range(NT):
-            lg = rows.tile([P, C], F32, name="lg")
-            logit.append(lg)
             for n in range(2):
+                cols = slice(512 * n, 512 * n + 512)
                 acc = psum.tile([P, 512], F32, tag="bank", name="acc")
                 for g in range(2):
                     nc.tensor.matmul_mx(
@@ -174,38 +168,34 @@ def tile_binarymlp_pb_kernel(tc, z2, g2, beta2, W3, b3, out):
                         start=(g == 0),
                         stop=(g == 1),
                     )
-                nc.vector.tensor_tensor(
-                    out=lg[:, 512 * n : 512 * n + 512], in0=acc[:], in1=bias[:, 512 * n : 512 * n + 512], op=ALU.add
-                )
-            nc.vector.tensor_reduce(out=negm[:, j : j + 1], in_=lg[:], axis=AX.X, op=ALU.max, negate=True)
+                nc.vector.tensor_tensor(out=lg[:, j, cols], in0=acc[:], in1=bias[:, cols], op=ALU.add)
+            nc.vector.tensor_reduce(out=negm[:, j : j + 1], in_=lg[:, j, :], axis=AX.X, op=ALU.max, negate=True)
             ex = junk.tile([P, C], BF16, name="ex")
             nc.scalar.activation(
-                out=ex[:], in_=lg[:], func=ACT.Exp, bias=negm[:, j : j + 1], scale=1.0,
+                out=ex[:], in_=lg[:, j, :], func=ACT.Exp, bias=negm[:, j : j + 1], scale=1.0,
                 accum_out=sums[:, j : j + 1],
             )
-            if j % 4 == 3:
-                gs = slice(j - 3, j + 1)
+            if j == FIRST_GROUP - 1:
+                gs = slice(0, FIRST_GROUP)
                 nc.scalar.activation(out=lns[:, gs], in_=sums[:, gs], func=ACT.Ln)
-                negc = negc_a if j == 3 else negc_b
-                if j == 3:
-                    nc.gpsimd.tensor_tensor(out=negc[:, gs], in0=negm[:, gs], in1=lns[:, gs], op=ALU.subtract)
-                    who = ["g", "g", "g", "g"]
-                else:
-                    nc.vector.tensor_tensor(out=negc[:, gs], in0=negm[:, gs], in1=lns[:, gs], op=ALU.subtract)
-                    who = ["v", "s", "g", "v"]
-                for a in range(4):
-                    i = j - 3 + a
-                    if who[a] == "g":
-                        nc.gpsimd.tensor_scalar(
-                            out=logit[i][:], in0=logit[i][:], scalar1=1.0, scalar2=negc[:, i : i + 1],
-                            op0=ALU.mult, op1=ALU.add,
-                        )
-                    elif who[a] == "v":
-                        nc.vector.tensor_scalar(
-                            out=logit[i][:], in0=logit[i][:], scalar1=negc[:, i : i + 1], scalar2=None, op0=ALU.add
-                        )
-                    else:
-                        nc.scalar.activation(
-                            out=logit[i][:], in_=logit[i][:], func=ACT.Identity, bias=negc[:, i : i + 1], scale=1.0
-                        )
-                    nc.sync.dma_start(out=out_view[i], in_=logit[i][:])
+                nc.gpsimd.tensor_tensor(out=negc_first[:, gs], in0=negm[:, gs], in1=lns[:, gs], op=ALU.subtract)
+                for i in range(FIRST_GROUP):
+                    nc.gpsimd.tensor_scalar(
+                        out=lg[:, i, :], in0=lg[:, i, :], scalar1=1.0, scalar2=negc_first[:, i : i + 1],
+                        op0=ALU.mult, op1=ALU.add,
+                    )
+                    nc.sync.dma_start(out=out_view[i], in_=lg[:, i, :])
+        gs = slice(FIRST_GROUP, NT)
+        nc.scalar.activation(out=lns[:, gs], in_=sums[:, gs], func=ACT.Ln)
+        nc.vector.tensor_tensor(out=negc_last[:, gs], in0=negm[:, gs], in1=lns[:, gs], op=ALU.subtract)
+        for i in range(FIRST_GROUP, NT):
+            shift = negc_last[:, i : i + 1]
+            if i % 3 == 0:
+                nc.scalar.activation(out=lg[:, i, :], in_=lg[:, i, :], func=ACT.Identity, bias=shift, scale=1.0)
+            elif i % 3 == 1:
+                nc.gpsimd.tensor_scalar(
+                    out=lg[:, i, :], in0=lg[:, i, :], scalar1=1.0, scalar2=shift, op0=ALU.mult, op1=ALU.add
+                )
+            else:
+                nc.vector.tensor_scalar(out=lg[:, i, :], in0=lg[:, i, :], scalar1=shift, scalar2=None, op0=ALU.add)
+            nc.sync.dma_start(out=out_view[i], in_=lg[:, i, :])

@@ -63,6 +63,7 @@ def tile_binarymlp_pb_kernel(tc, z2, g2, beta2, W3, b3, out):
         zw3 = zw[:].rearrange("p (v b) -> p v b", v=4)
         zwb = zw[:].bitcast(BF16)
         zw4 = zwb.rearrange("p (v b e) -> p v b e", v=4, e=2)
+        zp = keep.tile([P, 8, B], BF16, name="zp")
         st = keep.tile([P, 4, 4, 6], F32, name="st")
         for jj in range(4):
             for g in range(2):
@@ -79,9 +80,14 @@ def tile_binarymlp_pb_kernel(tc, z2, g2, beta2, W3, b3, out):
                     out=zw3[:, 2 * g : 2 * g + 2, 256 * jj : 256 * jj + 256],
                     in_=zbank[:].rearrange("p (u b) -> p u b", u=2),
                 )
-                for v in (2 * g, 2 * g + 1):
-                    lo = 2 * (v * B + 256 * jj)
-                    nc.vector.bn_stats(out=st[:, v, jj, :], in_=zwb[:, lo : lo + 512])
+                zb = zbank[:].bitcast(BF16)
+                for u in range(2):
+                    nc.vector.bn_stats(out=st[:, 2 * g + u, jj, :], in_=zb[:, 512 * u : 512 * u + 512])
+            for e in range(2):
+                nc.gpsimd.tensor_scalar(
+                    out=zp[:, e : 8 : 2, 256 * jj : 256 * jj + 256], in0=zw4[:, :, 256 * jj : 256 * jj + 256, e],
+                    scalar1=1.0, scalar2=0.0, op0=ALU.mult, op1=ALU.add,
+                )
 
         wg = keep.tile([P, 2 * C * 4], BF16, name="wg", align_bytes=64)
         wg_words = wg[:].bitcast(F32).rearrange("p (g c u) -> p g c u", g=2, u=2)
@@ -126,7 +132,7 @@ def tile_binarymlp_pb_kernel(tc, z2, g2, beta2, W3, b3, out):
                 for t in range(4):
                     c = 4 * g + t
                     nc.vector.tensor_scalar(
-                        out=hT[:, c, bs], in0=zw4[:, c // 2, bs, c % 2],
+                        out=hT[:, c, bs], in0=zp[:, c, bs],
                         scalar1=sc[:, c : c + 1], scalar2=bi[:, c : c + 1], op0=ALU.mult, op1=ALU.add,
                     )
                 lo = g * B + 512 * r

@@ -102,22 +102,27 @@ def tile_binarymlp_pb_kernel(tc, z2, g2, beta2, W3, b3, out):
             )
 
         mv = keep.tile([P, 8, 2], F32, name="mv")
-        vare = keep.tile([P, 8], F32, name="vare")
         std = keep.tile([P, 8], F32, name="std")
         rstd = keep.tile([P, 8], F32, name="rstd")
+        mg = keep.tile([P, 8], F32, name="mg")
         sc = keep.tile([P, 8], F32, name="sc")
         msc = keep.tile([P, 8], F32, name="msc")
         bi = keep.tile([P, 8], F32, name="bi")
+        halves = (slice(0, 4), slice(4, 8))
         for g in range(2):
-            cs = slice(4 * g, 4 * g + 4)
             for v in (2 * g, 2 * g + 1):
                 for e in range(2):
                     nc.vector.bn_aggr(out=mv[:, 2 * v + e, :], in_=st[:, v, :, 3 * e : 3 * e + 3])
-            nc.vector.tensor_scalar(out=vare[:, cs], in0=mv[:, cs, 1], scalar1=BN_EPS, scalar2=None, op0=ALU.add)
-            nc.scalar.activation(out=std[:, cs], in_=vare[:, cs], func=ACT.Sqrt)
+            nc.scalar.activation(out=std[:, halves[g]], in_=mv[:, halves[g], 1], func=ACT.Sqrt, bias=BN_EPS, scale=1.0)
+        for cs in halves:
+            nc.vector.tensor_tensor(out=mg[:, cs], in0=mv[:, cs, 0], in1=gamma[:, cs], op=ALU.mult)
+        for cs in halves:
             nc.vector.reciprocal(out=rstd[:, cs], in_=std[:, cs])
+        for cs in halves:
             nc.vector.tensor_tensor(out=sc[:, cs], in0=gamma[:, cs], in1=rstd[:, cs], op=ALU.mult)
-            nc.vector.tensor_tensor(out=msc[:, cs], in0=mv[:, cs, 0], in1=sc[:, cs], op=ALU.mult)
+        for cs in halves:
+            nc.vector.tensor_tensor(out=msc[:, cs], in0=mg[:, cs], in1=rstd[:, cs], op=ALU.mult)
+        for cs in halves:
             nc.vector.tensor_tensor(out=bi[:, cs], in0=beta[:, cs], in1=msc[:, cs], op=ALU.subtract)
 
         wq = keep.tile([P, 2 * C], U32, name="wq", align_bytes=64)
@@ -126,6 +131,12 @@ def tile_binarymlp_pb_kernel(tc, z2, g2, beta2, W3, b3, out):
         hg = keep.tile([P, 2 * B * 4], BF16, name="hg", align_bytes=64)
         hq = keep.tile([P, 2 * B], U32, name="hq", align_bytes=64)
         hs = keep.tile([P, 2 * B], U8, name="hs", align_bytes=64)
+        def quantise(codes, scales, grouped, lo):
+            nc.vector.quantize_mx(
+                out=codes[:, lo : lo + 512].bitcast(FP8X4), scales=scales[:, lo : lo + 512],
+                in_=grouped[:, 4 * lo : 4 * lo + 2048],
+            )
+
         for r in range(2):
             bs = slice(512 * r, 512 * r + 512)
             for g in range(2):
@@ -139,19 +150,15 @@ def tile_binarymlp_pb_kernel(tc, z2, g2, beta2, W3, b3, out):
                 dst = hg[:, 4 * lo : 4 * lo + 2048].rearrange("p (c i t) -> p c t i", i=4, t=4)
                 src = hT[:, 4 * g : 4 * g + 4, bs].rearrange("p t (c i) -> p c t i", i=4)
                 if r == 0 and g == 1:
+                    quantise(wq, ws, wg, 0)
                     nc.vector.tensor_scalar(out=dst, in0=src, scalar1=0.0, scalar2=None, op0=ALU.max)
                 else:
                     nc.scalar.activation(out=dst, in_=src, func=ACT.Relu)
+            if r == 1:
+                quantise(wq, ws, wg, 512)
+            quantise(wq, ws, wg, C + 512 * r)
             for g in range(2):
-                lo = g * C + 512 * r
-                nc.vector.quantize_mx(
-                    out=wq[:, lo : lo + 512].bitcast(FP8X4), scales=ws[:, lo : lo + 512], in_=wg[:, 4 * lo : 4 * lo + 2048]
-                )
-            for g in range(2):
-                lo = g * B + 512 * r
-                nc.vector.quantize_mx(
-                    out=hq[:, lo : lo + 512].bitcast(FP8X4), scales=hs[:, lo : lo + 512], in_=hg[:, 4 * lo : 4 * lo + 2048]
-                )
+                quantise(hq, hs, hg, g * B + 512 * r)
 
         lg = keep.tile([P, NT, C], F32, name="lg")
         negm = keep.tile([P, NT], F32, name="negm")
@@ -160,21 +167,23 @@ def tile_binarymlp_pb_kernel(tc, z2, g2, beta2, W3, b3, out):
         negc_first = keep.tile([P, NT], F32, name="negc_first")
         negc_last = keep.tile([P, NT], F32, name="negc_last")
         out_view = out.rearrange("(p t) c -> t p c", t=NT)
-        for j in range(NT):
-            for n in range(2):
-                cols = slice(512 * n, 512 * n + 512)
-                acc = psum.tile([P, 512], F32, tag="bank", name="acc")
-                for g in range(2):
-                    nc.tensor.matmul_mx(
-                        out=acc[:],
-                        lhsT=hq[:, g * B + P * j : g * B + P * j + P].bitcast(FP8X4),
-                        lhsT_scale=hs[:, g * B + P * j : g * B + P * j + P],
-                        rhs=wq[:, g * C + 512 * n : g * C + 512 * n + 512].bitcast(FP8X4),
-                        rhs_scale=ws[:, g * C + 512 * n : g * C + 512 * n + 512],
-                        start=(g == 0),
-                        stop=(g == 1),
-                    )
-                nc.vector.tensor_tensor(out=lg[:, j, cols], in0=acc[:], in1=bias[:, cols], op=ALU.add)
+
+        def logits(j, n):
+            cols = slice(512 * n, 512 * n + 512)
+            acc = psum.tile([P, 512], F32, tag="bank", name="acc")
+            for g in range(2):
+                nc.tensor.matmul_mx(
+                    out=acc[:],
+                    lhsT=hq[:, g * B + P * j : g * B + P * j + P].bitcast(FP8X4),
+                    lhsT_scale=hs[:, g * B + P * j : g * B + P * j + P],
+                    rhs=wq[:, g * C + 512 * n : g * C + 512 * n + 512].bitcast(FP8X4),
+                    rhs_scale=ws[:, g * C + 512 * n : g * C + 512 * n + 512],
+                    start=(g == 0),
+                    stop=(g == 1),
+                )
+            nc.vector.tensor_tensor(out=lg[:, j, cols], in0=acc[:], in1=bias[:, cols], op=ALU.add)
+
+        def exponentials(j):
             nc.vector.tensor_reduce(out=negm[:, j : j + 1], in_=lg[:, j, :], axis=AX.X, op=ALU.max, negate=True)
             ex = junk.tile([P, C], BF16, name="ex")
             nc.scalar.activation(
@@ -191,6 +200,13 @@ def tile_binarymlp_pb_kernel(tc, z2, g2, beta2, W3, b3, out):
                         op0=ALU.mult, op1=ALU.add,
                     )
                     nc.sync.dma_start(out=out_view[i], in_=lg[:, i, :])
+
+        for j in range(NT):
+            logits(j, 0)
+            if j > 0:
+                exponentials(j - 1)
+            logits(j, 1)
+        exponentials(NT - 1)
         gs = slice(FIRST_GROUP, NT)
         nc.scalar.activation(out=lns[:, gs], in_=sums[:, gs], func=ACT.Ln)
         nc.vector.tensor_tensor(out=negc_last[:, gs], in0=negm[:, gs], in1=lns[:, gs], op=ALU.subtract)

@@ -20,6 +20,7 @@ K = 1024
 C = 1024
 NT = B // P
 BN_EPS = 1e-5
+WARM_UP = 6
 FIRST_GROUP = 5
 
 
@@ -32,6 +33,8 @@ def tile_binarymlp_pb_kernel(tc, z2, g2, beta2, W3, b3, out):
 
         ident = keep.tile([P, P], F32, name="ident")
         make_identity(nc, ident[:])
+        ident_bf = keep.tile([P, P], BF16, name="ident_bf")
+        make_identity(nc, ident_bf[:])
         one = keep.tile([P, 1], F32, name="one")
         nc.vector.memset(one[:], 1.0)
         warm = keep.tile([P, 1], F32, name="warm")
@@ -114,6 +117,7 @@ def tile_binarymlp_pb_kernel(tc, z2, g2, beta2, W3, b3, out):
                 for e in range(2):
                     nc.vector.bn_aggr(out=mv[:, 2 * v + e, :], in_=st[:, v, :, 3 * e : 3 * e + 3])
             nc.scalar.activation(out=std[:, halves[g]], in_=mv[:, halves[g], 1], func=ACT.Sqrt, bias=BN_EPS, scale=1.0)
+        nc.scalar.activation(out=warm[:], in_=std[:, 7:8], func=ACT.Exp, scale=0.0)
         for cs in halves:
             nc.vector.tensor_tensor(out=mg[:, cs], in0=mv[:, cs, 0], in1=gamma[:, cs], op=ALU.mult)
         for cs in halves:
@@ -149,6 +153,10 @@ def tile_binarymlp_pb_kernel(tc, z2, g2, beta2, W3, b3, out):
                 lo = g * B + 512 * r
                 dst = hg[:, 4 * lo : 4 * lo + 2048].rearrange("p (c i t) -> p c t i", i=4, t=4)
                 src = hT[:, 4 * g : 4 * g + 4, bs].rearrange("p t (c i) -> p c t i", i=4)
+                if r == 0 and g == 0:
+                    heat = psum.tile([P, 512], F32, tag="bank", name="heat")
+                    for t in range(WARM_UP):
+                        nc.tensor.matmul(heat[:], lhsT=ident_bf[:], rhs=hT[:, t % 4, bs], start=True, stop=True)
                 if r == 0 and g == 1:
                     quantise(wq, ws, wg, 0)
                     nc.vector.tensor_scalar(out=dst, in0=src, scalar1=0.0, scalar2=None, op0=ALU.max)

from contextlib import ExitStack

import concourse.mybir as mybir
from concourse.masks import make_identity

FLOPS = 2 * 1024 * 1024 * 1024

F32 = mybir.dt.float32
BF16 = mybir.dt.bfloat16
U32 = mybir.dt.uint32
U8 = mybir.dt.uint8
FP8X4 = mybir.dt.float8_e4m3fn_x4
ALU = mybir.AluOpType
ACT = mybir.ActivationFunctionType
AX = mybir.AxisListType

P = 128
B = 1024
K = 1024
C = 1024
NT = B // P
BN_EPS = 1e-5
WARM_UP = 6
FIRST_GROUP = 5


def tile_binarymlp_pb_kernel(tc, z2, g2, beta2, W3, b3, out):
    nc = tc.nc
    with ExitStack() as ctx:
        keep = ctx.enter_context(tc.tile_pool(name="keep", bufs=1))
        junk = ctx.enter_context(tc.tile_pool(name="junk", bufs=2))
        psum = ctx.enter_context(tc.psum_pool(name="psum", bufs=8))

        ident = keep.tile([P, P], F32, name="ident")
        make_identity(nc, ident[:])
        ident_bf = keep.tile([P, P], BF16, name="ident_bf")
        make_identity(nc, ident_bf[:])
        one = keep.tile([P, 1], F32, name="one")
        nc.vector.memset(one[:], 1.0)
        warm = keep.tile([P, 1], F32, name="warm")
        nc.scalar.activation(out=warm[:], in_=one[:], func=ACT.Sqrt)

        z_nat = keep.tile([P, NT, K], BF16, name="z_nat")
        z_view = z2.rearrange("(p t) f -> p t f", t=NT)
        for g in range(2):
            nc.sync.dma_start(out=z_nat[:, 0:2, 512 * g : 512 * g + 512], in_=z_view[:, 0:2, 512 * g : 512 * g + 512])
        for c in range(1, 4):
            nc.sync.dma_start(out=z_nat[:, 2 * c : 2 * c + 2, :], in_=z_view[:, 2 * c : 2 * c + 2, :])
        gamma = keep.tile([P, 8], BF16, name="gamma")
        beta = keep.tile([P, 8], BF16, name="beta")
        with nc.allow_non_contiguous_dma(reason="two small vectors, a pair of features to a partition"):
            nc.sync.dma_start(
                out=gamma[:].rearrange("p (v e) -> p v e", e=2), in_=g2.rearrange("(v q e) -> q v e", v=4, e=2)
            )
            nc.sync.dma_start(
                out=beta[:].rearrange("p (v e) -> p v e", e=2), in_=beta2.rearrange("(v q e) -> q v e", v=4, e=2)
            )
        w_nat = keep.tile([P, NT, K], BF16, name="w_nat")
        w_view = W3.rearrange("(j p) f -> p j f", p=P)
        for c in range(4):
            nc.sync.dma_start(out=w_nat[:, 2 * c : 2 * c + 2, :], in_=w_view[:, 2 * c : 2 * c + 2, :])
        bias = keep.tile([P, C], BF16, name="bias")
        nc.sync.dma_start(out=bias[:], in_=b3.partition_broadcast(P))

        zw = keep.tile([P, 4 * B], F32, name="zw")
        zw3 = zw[:].rearrange("p (v b) -> p v b", v=4)
        zwb = zw[:].bitcast(BF16)
        zw4 = zwb.rearrange("p (v b e) -> p v b e", v=4, e=2)
        zp = keep.tile([P, 8, B], BF16, name="zp")
        st = keep.tile([P, 4, 4, 6], F32, name="st")
        for jj in range(4):
            for g in range(2):
                zbank = psum.tile([P, 512], F32, tag="bank", name="zbank")
                for u in range(2):
                    for jl in range(2):
                        v = 2 * g + u
                        nc.tensor.transpose(
                            zbank[:, 256 * u + P * jl : 256 * u + P * jl + P],
                            z_nat[:, 2 * jj + jl, :].bitcast(F32)[:, P * v : P * v + P],
                            ident[:],
                        )
                nc.scalar.copy(
                    out=zw3[:, 2 * g : 2 * g + 2, 256 * jj : 256 * jj + 256],
                    in_=zbank[:].rearrange("p (u b) -> p u b", u=2),
                )
                zb = zbank[:].bitcast(BF16)
                for u in range(2):
                    nc.vector.bn_stats(out=st[:, 2 * g + u, jj, :], in_=zb[:, 512 * u : 512 * u + 512])
            for e in range(2):
                nc.gpsimd.tensor_scalar(
                    out=zp[:, e : 8 : 2, 256 * jj : 256 * jj + 256], in0=zw4[:, :, 256 * jj : 256 * jj + 256, e],
                    scalar1=1.0, scalar2=0.0, op0=ALU.mult, op1=ALU.add,
                )

        wg = keep.tile([P, 2 * C * 4], BF16, name="wg", align_bytes=64)
        wg_words = wg[:].bitcast(F32).rearrange("p (g c u) -> p g c u", g=2, u=2)
        for j in range(NT):
            wbank = psum.tile([P, 512], F32, tag="bank", name="wbank")
            for v in range(4):
                nc.tensor.transpose(
                    wbank[:, P * v : P * v + P], w_nat[:, j, :].bitcast(F32)[:, P * v : P * v + P], ident[:]
                )
            nc.scalar.copy(
                out=wg_words[:, :, P * j : P * j + P, :], in_=wbank[:].rearrange("p (g u c) -> p g c u", g=2, u=2)
            )

        mv = keep.tile([P, 8, 2], F32, name="mv")
        std = keep.tile([P, 8], F32, name="std")
        rstd = keep.tile([P, 8], F32, name="rstd")
        mg = keep.tile([P, 8], F32, name="mg")
        sc = keep.tile([P, 8], F32, name="sc")
        msc = keep.tile([P, 8], F32, name="msc")
        bi = keep.tile([P, 8], F32, name="bi")
        halves = (slice(0, 4), slice(4, 8))
        for g in range(2):
            for v in (2 * g, 2 * g + 1):
                for e in range(2):
                    nc.vector.bn_aggr(out=mv[:, 2 * v + e, :], in_=st[:, v, :, 3 * e : 3 * e + 3])
            nc.scalar.activation(out=std[:, halves[g]], in_=mv[:, halves[g], 1], func=ACT.Sqrt, bias=BN_EPS, scale=1.0)
        nc.scalar.activation(out=warm[:], in_=std[:, 7:8], func=ACT.Exp, scale=0.0)
        for cs in halves:
            nc.vector.tensor_tensor(out=mg[:, cs], in0=mv[:, cs, 0], in1=gamma[:, cs], op=ALU.mult)
        for cs in halves:
            nc.vector.reciprocal(out=rstd[:, cs], in_=std[:, cs])
        for cs in halves:
            nc.vector.tensor_tensor(out=sc[:, cs], in0=gamma[:, cs], in1=rstd[:, cs], op=ALU.mult)
        for cs in halves:
            nc.vector.tensor_tensor(out=msc[:, cs], in0=mg[:, cs], in1=rstd[:, cs], op=ALU.mult)
        for cs in halves:
            nc.vector.tensor_tensor(out=bi[:, cs], in0=beta[:, cs], in1=msc[:, cs], op=ALU.subtract)

        wq = keep.tile([P, 2 * C], U32, name="wq", align_bytes=64)
        ws = keep.tile([P, 2 * C], U8, name="ws", align_bytes=64)
        hT = keep.tile([P, 8, B], BF16, name="hT")
        hg = keep.tile([P, 2 * B * 4], BF16, name="hg", align_bytes=64)
        hq = keep.tile([P, 2 * B], U32, name="hq", align_bytes=64)
        hs = keep.tile([P, 2 * B], U8, name="hs", align_bytes=64)
        def quantise(codes, scales, grouped, lo):
            nc.vector.quantize_mx(
                out=codes[:, lo : lo + 512].bitcast(FP8X4), scales=scales[:, lo : lo + 512],
                in_=grouped[:, 4 * lo : 4 * lo + 2048],
            )

        for r in range(2):
            bs = slice(512 * r, 512 * r + 512)
            for g in range(2):
                for t in range(4):
                    c = 4 * g + t
                    nc.vector.tensor_scalar(
                        out=hT[:, c, bs], in0=zp[:, c, bs],
                        scalar1=sc[:, c : c + 1], scalar2=bi[:, c : c + 1], op0=ALU.mult, op1=ALU.add,
                    )
                lo = g * B + 512 * r
                dst = hg[:, 4 * lo : 4 * lo + 2048].rearrange("p (c i t) -> p c t i", i=4, t=4)
                src = hT[:, 4 * g : 4 * g + 4, bs].rearrange("p t (c i) -> p c t i", i=4)
                if r == 0 and g == 0:
                    heat = psum.tile([P, 512], F32, tag="bank", name="heat")
                    for t in range(WARM_UP):
                        nc.tensor.matmul(heat[:], lhsT=ident_bf[:], rhs=hT[:, t % 4, bs], start=True, stop=True)
                if r == 0 and g == 1:
                    quantise(wq, ws, wg, 0)
                    nc.vector.tensor_scalar(out=dst, in0=src, scalar1=0.0, scalar2=None, op0=ALU.max)
                else:
                    nc.scalar.activation(out=dst, in_=src, func=ACT.Relu)
            if r == 1:
                quantise(wq, ws, wg, 512)
            quantise(wq, ws, wg, C + 512 * r)
            for g in range(2):
                quantise(hq, hs, hg, g * B + 512 * r)

        lg = keep.tile([P, NT, C], F32, name="lg")
        negm = keep.tile([P, NT], F32, name="negm")
        sums = keep.tile([P, NT], F32, name="sums")
        lns = keep.tile([P, NT], F32, name="lns")
        negc_first = keep.tile([P, NT], F32, name="negc_first")
        negc_last = keep.tile([P, NT], F32, name="negc_last")
        out_view = out.rearrange("(p t) c -> t p c", t=NT)

        def logits(j, n):
            cols = slice(512 * n, 512 * n + 512)
            acc = psum.tile([P, 512], F32, tag="bank", name="acc")
            for g in range(2):
                nc.tensor.matmul_mx(
                    out=acc[:],
                    lhsT=hq[:, g * B + P * j : g * B + P * j + P].bitcast(FP8X4),
                    lhsT_scale=hs[:, g * B + P * j : g * B + P * j + P],
                    rhs=wq[:, g * C + 512 * n : g * C + 512 * n + 512].bitcast(FP8X4),
                    rhs_scale=ws[:, g * C + 512 * n : g * C + 512 * n + 512],
                    start=(g == 0),
                    stop=(g == 1),
                )
            nc.vector.tensor_tensor(out=lg[:, j, cols], in0=acc[:], in1=bias[:, cols], op=ALU.add)

        def exponentials(j):
            nc.vector.tensor_reduce(out=negm[:, j : j + 1], in_=lg[:, j, :], axis=AX.X, op=ALU.max, negate=True)
            ex = junk.tile([P, C], BF16, name="ex")
            nc.scalar.activation(
                out=ex[:], in_=lg[:, j, :], func=ACT.Exp, bias=negm[:, j : j + 1], scale=1.0,
                accum_out=sums[:, j : j + 1],
            )
            if j == FIRST_GROUP - 1:
                gs = slice(0, FIRST_GROUP)
                nc.scalar.activation(out=lns[:, gs], in_=sums[:, gs], func=ACT.Ln)
                nc.gpsimd.tensor_tensor(out=negc_first[:, gs], in0=negm[:, gs], in1=lns[:, gs], op=ALU.subtract)
                for i in range(FIRST_GROUP):
                    nc.gpsimd.tensor_scalar(
                        out=lg[:, i, :], in0=lg[:, i, :], scalar1=1.0, scalar2=negc_first[:, i : i + 1],
                        op0=ALU.mult, op1=ALU.add,
                    )
                    nc.sync.dma_start(out=out_view[i], in_=lg[:, i, :])

        for j in range(NT):
            logits(j, 0)
            if j > 0:
                exponentials(j - 1)
            logits(j, 1)
        exponentials(NT - 1)
        gs = slice(FIRST_GROUP, NT)
        nc.scalar.activation(out=lns[:, gs], in_=sums[:, gs], func=ACT.Ln)
        nc.vector.tensor_tensor(out=negc_last[:, gs], in0=negm[:, gs], in1=lns[:, gs], op=ALU.subtract)
        for i in range(FIRST_GROUP, NT):
            shift = negc_last[:, i : i + 1]
            if i % 3 == 0:
                nc.scalar.activation(out=lg[:, i, :], in_=lg[:, i, :], func=ACT.Identity, bias=shift, scale=1.0)
            elif i % 3 == 1:
                nc.gpsimd.tensor_scalar(
                    out=lg[:, i, :], in0=lg[:, i, :], scalar1=1.0, scalar2=shift, op0=ALU.mult, op1=ALU.add
                )
            else:
                nc.vector.tensor_scalar(out=lg[:, i, :], in0=lg[:, i, :], scalar1=shift, scalar2=None, op0=ALU.add)
            nc.sync.dma_start(out=out_view[i], in_=lg[:, i, :])
